import numpy as np
import ml_dtypes


def mxq(x, axis, fmt="e4m3"):
    dtype, down = {"e4m3": (ml_dtypes.float8_e4m3fn, 7), "e5m2": (ml_dtypes.float8_e5m2, 14)}[fmt]
    v = np.moveaxis(np.asarray(x, np.float32).astype(ml_dtypes.bfloat16).astype(np.float64), axis, -1)
    blocks = v.reshape(v.shape[:-1] + (-1, 32))
    amax = np.abs(blocks).max(-1, keepdims=True)
    byte = np.maximum(np.where(amax > 0, np.frexp(amax)[1] - 1 + 127, 0) - down, 1)
    scale = np.exp2(byte - 127.0)
    codes = (blocks / scale).astype(np.float32).astype(dtype).astype(np.float64)
    return np.moveaxis((codes * scale).reshape(v.shape), -1, axis)


WIDE = False


def mx_kscale(k):
    if not WIDE:
        return np.ones(k)
    levels = np.array([10, -10, 5, -5, 0])
    a = np.random.permutation(np.resize(levels, k // 512 * 4)).reshape(k // 512, 4)
    idx = np.arange(k)
    return np.exp2(a[idx // 512, idx % 128 // 32])


BF16 = ml_dtypes.bfloat16


def bf(x):
    return np.asarray(x, np.float32).astype(BF16)


def f64(x):
    return np.asarray(x).astype(np.float64)


N, NK, D_IN, D_H, D_V = 1024, 1024, 512, 512, 512


def setup_inputs():
    s = mx_kscale(D_H)
    return {
        "q": bf(np.random.standard_normal((N, D_H)) * 1.4 * s),
        "k": bf(np.random.standard_normal((N, D_H)) * 1.4 / s),
        "h": bf(np.random.standard_normal((N, D_H)) * 1.1),
        "cooccur": bf(np.random.standard_normal((N, N)) * 0.5 / np.sqrt(N)),
        "wv": bf(np.random.standard_normal((D_H, D_H)) * 0.9 / np.sqrt(D_H)),
        "bv": bf(np.random.standard_normal(D_H) * 0.3),
    }


def reference(q, k, h, cooccur, wv, bv):
    hf = f64(h)
    v = (mxq(hf, 1, "e4m3") @ mxq(f64(wv), 1, "e4m3").T) + f64(bv)
    sc = (mxq(f64(q), 1, "e4m3") @ mxq(f64(k), 1, "e4m3").T) * (1.0 / np.sqrt(D_H))
    e = np.exp(sc - sc.max(-1, keepdims=True))
    att = e / e.sum(-1, keepdims=True) + f64(cooccur)
    return np.maximum(mxq(att, 1, "e4m3") @ mxq(v, 0, "e4m3"), 0.0) + hf

@@ -1,0 +1,226 @@
+from contextlib import ExitStack
+import math
+
+import concourse.mybir as mybir
+from concourse.masks import make_identity
+
+F32 = mybir.dt.float32
+BF16 = mybir.dt.bfloat16
+U32 = mybir.dt.uint32
+U8 = mybir.dt.uint8
+FP8X4 = mybir.dt.float8_e4m3fn_x4
+ALU = mybir.AluOpType
+ACT = mybir.ActivationFunctionType
+AXIS = mybir.AxisListType
+
+P = 128
+PACK = 4
+K_PASS = P * PACK
+NODES = 1024
+FEATS = 512
+NODE_TILES = NODES // P
+FEAT_TILES = FEATS // P
+KEY_PASSES = NODES // K_PASS
+SCORE_SCALE = 1.0 / math.sqrt(FEATS)
+
+FLOPS = 2 * NODES * FEATS * FEATS + 2 * NODES * NODES * FEATS + 2 * NODES * NODES * FEATS
+
+
+def load_row_tiles(nc, rows_sb, rows, n_tiles):
+    for first in range(0, n_tiles, 2):
+        nc.sync.dma_start(
+            out=rows_sb[:, first : first + 2, :],
+            in_=rows[first * P : (first + 2) * P, :].rearrange("(t p) f -> p t f", p=P),
+        )
+
+
+def quantise_along_features(nc, psum, ident_f32, rows_sb, n_tiles, grouped, codes, scales):
+    grouped_words = grouped[:].bitcast(F32)
+    for pair in range(n_tiles // 2):
+        flipped = psum.tile([P, 2, 2, P], F32, tag="sc")
+        for j in range(2):
+            words = rows_sb[:, 2 * pair + j, :].bitcast(F32)
+            for u in range(2):
+                nc.tensor.transpose(flipped[:, j, u, :], words[:, u * P : (u + 1) * P], ident_f32[:])
+        first = 2 * pair * P
+        nc.scalar.copy(
+            out=grouped_words[:, 2 * first : 2 * (first + 2 * P)].rearrange("p (j n u) -> p j n u", j=2, u=2),
+            in_=flipped[:].rearrange("p j u n -> p j n u"),
+        )
+        nc.vector.quantize_mx(
+            out=codes[:, first : first + 2 * P].bitcast(FP8X4),
+            scales=scales[:, first : first + 2 * P],
+            in_=grouped[:, PACK * first : PACK * (first + 2 * P)],
+        )
+
+
+def tile_semanticgraph_pb_kernel(tc, q, k, h, cooccur, wv, bv, out):
+    nc = tc.nc
+    with ExitStack() as ctx:
+        const = ctx.enter_context(tc.tile_pool(name="const", bufs=1))
+        keep = ctx.enter_context(tc.tile_pool(name="keep", bufs=1))
+        work = ctx.enter_context(tc.tile_pool(name="work", bufs=3))
+        psum_sc = ctx.enter_context(tc.psum_pool(name="psum_sc", bufs=4))
+        psum_tp = ctx.enter_context(tc.psum_pool(name="psum_tp", bufs=2))
+        psum_acc = ctx.enter_context(tc.psum_pool(name="psum_acc", bufs=2))
+
+        wv_sb = keep.tile([P, FEAT_TILES, FEATS], BF16)
+        h_sb = keep.tile([P, NODE_TILES, FEATS], BF16)
+        k_sb = keep.tile([P, NODE_TILES, FEATS], BF16)
+        q_sb = keep.tile([P, NODE_TILES, FEATS], BF16)
+        prior_sb = keep.tile([P, NODE_TILES, NODES], BF16)
+        bias_sb = const.tile([P, FEATS], BF16)
+        nc.scalar.dma_start(out=bias_sb[:], in_=bv.partition_broadcast(P))
+        load_row_tiles(nc, wv_sb, wv, FEAT_TILES)
+        load_row_tiles(nc, h_sb, h, NODE_TILES)
+        load_row_tiles(nc, k_sb, k, NODE_TILES)
+        load_row_tiles(nc, q_sb, q, NODE_TILES)
+        for i in range(NODE_TILES):
+            nc.sync.dma_start(out=prior_sb[:, i, :], in_=cooccur[i * P : (i + 1) * P, :])
+
+        ident_f32 = const.tile([P, P], F32)
+        make_identity(nc, ident_f32[:])
+        ident_bf16 = const.tile([P, P], BF16)
+        make_identity(nc, ident_bf16[:])
+        warm = const.tile([P, 1], F32)
+        nc.vector.memset(warm[:], 0.0)
+        nc.scalar.activation(out=warm[:], in_=warm[:], func=ACT.Exp)
+
+        wv_grouped = keep.tile([P, PACK * FEATS], BF16, align_bytes=64)
+        wv_codes = keep.tile([P, FEATS], U32, align_bytes=64)
+        wv_scales = keep.tile([P, FEATS], U8, align_bytes=64)
+        quantise_along_features(nc, psum_sc, ident_f32, wv_sb, FEAT_TILES, wv_grouped, wv_codes, wv_scales)
+        h_grouped = keep.tile([P, PACK * NODES], BF16, align_bytes=64)
+        h_codes = keep.tile([P, NODES], U32, align_bytes=64)
+        h_scales = keep.tile([P, NODES], U8, align_bytes=64)
+        quantise_along_features(nc, psum_sc, ident_f32, h_sb, NODE_TILES, h_grouped, h_codes, h_scales)
+
+        v_grouped = keep.tile([P, KEY_PASSES, FEATS, PACK], BF16, align_bytes=64)
+        v_codes = keep.tile([P, KEY_PASSES, FEATS], U32, align_bytes=64)
+        v_scales = keep.tile([P, KEY_PASSES, FEATS], U8, align_bytes=64)
+        for g in range(KEY_PASSES):
+            for c in range(FEAT_TILES):
+                feats = slice(c * P, (c + 1) * P)
+                v_bank = psum_acc.tile([P, PACK, P], F32, tag="acc")
+                for t in range(PACK):
+                    nodes = slice((PACK * g + t) * P, (PACK * g + t + 1) * P)
+                    nc.tensor.matmul_mx(
+                        out=v_bank[:, t, :],
+                        lhsT=h_codes[:, nodes].bitcast(FP8X4),
+                        lhsT_scale=h_scales[:, nodes],
+                        rhs=wv_codes[:, feats].bitcast(FP8X4),
+                        rhs_scale=wv_scales[:, feats],
+                        start=True,
+                        stop=True,
+                    )
+                nc.vector.tensor_tensor(
+                    out=v_grouped[:, g, feats, :],
+                    in0=v_bank[:].rearrange("p t f -> p f t"),
+                    in1=bias_sb[:, feats].unsqueeze(2).to_broadcast([P, P, PACK]),
+                    op=ALU.add,
+                )
+            nc.vector.quantize_mx(
+                out=v_codes[:, g, :].bitcast(FP8X4),
+                scales=v_scales[:, g, :],
+                in_=v_grouped[:, g, :, :].rearrange("p f t -> p (f t)"),
+            )
+
+        k_grouped = keep.tile([P, PACK * NODES], BF16, align_bytes=64)
+        k_codes = keep.tile([P, NODES], U32, align_bytes=64)
+        k_scales = keep.tile([P, NODES], U8, align_bytes=64)
+        quantise_along_features(nc, psum_sc, ident_f32, k_sb, NODE_TILES, k_grouped, k_codes, k_scales)
+        q_grouped = keep.tile([P, PACK * NODES], BF16, align_bytes=64)
+        q_codes = keep.tile([P, NODES], U32, align_bytes=64)
+        q_scales = keep.tile([P, NODES], U8, align_bytes=64)
+        quantise_along_features(nc, psum_sc, ident_f32, q_sb, NODE_TILES, q_grouped, q_codes, q_scales)
+
+        for i in range(NODE_TILES):
+            queries = slice(i * P, (i + 1) * P)
+
+            score_banks = []
+            row_max = work.tile([P, KEY_PASSES], F32)
+            for g in range(KEY_PASSES):
+                keys = slice(g * K_PASS, (g + 1) * K_PASS)
+                score = psum_sc.tile([P, K_PASS], F32, tag="sc")
+                nc.tensor.matmul_mx(
+                    out=score[:],
+                    lhsT=q_codes[:, queries].bitcast(FP8X4),
+                    lhsT_scale=q_scales[:, queries],
+                    rhs=k_codes[:, keys].bitcast(FP8X4),
+                    rhs_scale=k_scales[:, keys],
+                    start=True,
+                    stop=True,
+                )
+                nc.vector.tensor_reduce(out=row_max[:, g : g + 1], in_=score[:], axis=AXIS.X, op=ALU.max)
+                score_banks.append(score)
+
+            shift = work.tile([P, 1], F32)
+            nc.vector.tensor_scalar(
+                out=shift[:],
+                in0=row_max[:, 0:1],
+                scalar1=row_max[:, 1:2],
+                scalar2=-SCORE_SCALE,
+                op0=ALU.max,
+                op1=ALU.mult,
+            )
+            expo = work.tile([P, NODES], F32)
+            row_sum = work.tile([P, KEY_PASSES], F32)
+            for g in range(KEY_PASSES):
+                nc.scalar.activation(
+                    out=expo[:, g * K_PASS : (g + 1) * K_PASS],
+                    in_=score_banks[g][:],
+                    func=ACT.Exp,
+                    bias=shift[:],
+                    scale=SCORE_SCALE,
+                    accum_out=row_sum[:, g : g + 1],
+                )
+            total = work.tile([P, 1], F32)
+            nc.vector.tensor_tensor(out=total[:], in0=row_sum[:, 0:1], in1=row_sum[:, 1:2], op=ALU.add)
+            inverse = work.tile([P, 1], F32)
+            nc.vector.reciprocal(out=inverse[:], in_=total[:])
+
+            att = work.tile([P, NODES], BF16)
+            att_grouped = work.tile([P, KEY_PASSES, P, PACK], BF16, align_bytes=64)
+            att_codes = work.tile([P, KEY_PASSES, P], U32, align_bytes=64)
+            att_scales = work.tile([P, KEY_PASSES, P], U8, align_bytes=64)
+            result = psum_acc.tile([P, FEATS], F32, tag="acc")
+            for g in range(KEY_PASSES):
+                keys = slice(g * K_PASS, (g + 1) * K_PASS)
+                nc.vector.scalar_tensor_tensor(
+                    out=att[:, keys],
+                    in0=expo[:, keys],
+                    scalar=inverse[:],
+                    in1=prior_sb[:, i, keys],
+                    op0=ALU.mult,
+                    op1=ALU.add,
+                )
+                att_flipped = psum_tp.tile([P, PACK, P], BF16, tag="tp")
+                for t in range(PACK):
+                    first = g * K_PASS + t * P
+                    nc.tensor.transpose(att_flipped[:, t, :], att[:, first : first + P], ident_bf16[:])
+                nc.scalar.copy(out=att_grouped[:, g, :, :], in_=att_flipped[:].rearrange("p t r -> p r t"))
+                nc.vector.quantize_mx(
+                    out=att_codes[:, g, :].bitcast(FP8X4),
+                    scales=att_scales[:, g, :],
+                    in_=att_grouped[:, g, :, :].rearrange("p r t -> p (r t)"),
+                )
+                nc.tensor.matmul_mx(
+                    out=result[:],
+                    lhsT=att_codes[:, g, :].bitcast(FP8X4),
+                    lhsT_scale=att_scales[:, g, :],
+                    rhs=v_codes[:, g, :].bitcast(FP8X4),
+                    rhs_scale=v_scales[:, g, :],
+                    start=(g == 0),
+                    stop=(g == KEY_PASSES - 1),
+                )
+
+            out_sb = work.tile([P, FEATS], F32)
+            nc.vector.scalar_tensor_tensor(
+                out=out_sb[:],
+                in0=result[:],
+                scalar=0.0,
+                in1=h_sb[:, i, :],
+                op0=ALU.max,
+                op1=ALU.add,
+            )
+            nc.sync.dma_start(out=out[queries, :], in_=out_sb[:])

@@ -6,6 +6,7 @@ from concourse.masks import make_identity
 
 F32 = mybir.dt.float32
 BF16 = mybir.dt.bfloat16
+I32 = mybir.dt.int32
 U32 = mybir.dt.uint32
 U8 = mybir.dt.uint8
 FP8X4 = mybir.dt.float8_e4m3fn_x4
@@ -26,34 +27,6 @@ SCORE_SCALE = 1.0 / math.sqrt(FEATS)
 FLOPS = 2 * NODES * FEATS * FEATS + 2 * NODES * NODES * FEATS + 2 * NODES * NODES * FEATS
 
 
-def load_row_tiles(nc, rows_sb, rows, n_tiles):
-    for first in range(0, n_tiles, 2):
-        nc.sync.dma_start(
-            out=rows_sb[:, first : first + 2, :],
-            in_=rows[first * P : (first + 2) * P, :].rearrange("(t p) f -> p t f", p=P),
-        )
-
-
-def quantise_along_features(nc, psum, ident_f32, rows_sb, n_tiles, grouped, codes, scales):
-    grouped_words = grouped[:].bitcast(F32)
-    for pair in range(n_tiles // 2):
-        flipped = psum.tile([P, 2, 2, P], F32, tag="sc")
-        for j in range(2):
-            words = rows_sb[:, 2 * pair + j, :].bitcast(F32)
-            for u in range(2):
-                nc.tensor.transpose(flipped[:, j, u, :], words[:, u * P : (u + 1) * P], ident_f32[:])
-        first = 2 * pair * P
-        nc.scalar.copy(
-            out=grouped_words[:, 2 * first : 2 * (first + 2 * P)].rearrange("p (j n u) -> p j n u", j=2, u=2),
-            in_=flipped[:].rearrange("p j u n -> p j n u"),
-        )
-        nc.vector.quantize_mx(
-            out=codes[:, first : first + 2 * P].bitcast(FP8X4),
-            scales=scales[:, first : first + 2 * P],
-            in_=grouped[:, PACK * first : PACK * (first + 2 * P)],
-        )
-
-
 def tile_semanticgraph_pb_kernel(tc, q, k, h, cooccur, wv, bv, out):
     nc = tc.nc
     with ExitStack() as ctx:
@@ -63,18 +36,27 @@ def tile_semanticgraph_pb_kernel(tc, q, k, h, cooccur, wv, bv, out):
         psum_sc = ctx.enter_context(tc.psum_pool(name="psum_sc", bufs=4))
         psum_tp = ctx.enter_context(tc.psum_pool(name="psum_tp", bufs=2))
         psum_acc = ctx.enter_context(tc.psum_pool(name="psum_acc", bufs=2))
+        ctx.enter_context(tc.manual_schedule())
 
+        def load_row_tiles(rows_sb, rows, n_tiles):
+            for first in range(0, n_tiles, 2):
+                nc.sync.dma_start(
+                    out=rows_sb[:, first : first + 2, :],
+                    in_=rows[first * P : (first + 2) * P, :].rearrange("(t p) f -> p t f", p=P),
+                )
+
+        bias_row = const.tile([P, FEATS], BF16)
+        nc.vector.memset(bias_row[:].bitcast(I32), 0)
+        nc.scalar.dma_start(out=bias_row[0:1, :], in_=bv.rearrange("(o f) -> o f", o=1))
         wv_sb = keep.tile([P, FEAT_TILES, FEATS], BF16)
         h_sb = keep.tile([P, NODE_TILES, FEATS], BF16)
         k_sb = keep.tile([P, NODE_TILES, FEATS], BF16)
         q_sb = keep.tile([P, NODE_TILES, FEATS], BF16)
         prior_sb = keep.tile([P, NODE_TILES, NODES], BF16)
-        bias_sb = const.tile([P, FEATS], BF16)
-        nc.scalar.dma_start(out=bias_sb[:], in_=bv.partition_broadcast(P))
-        load_row_tiles(nc, wv_sb, wv, FEAT_TILES)
-        load_row_tiles(nc, h_sb, h, NODE_TILES)
-        load_row_tiles(nc, k_sb, k, NODE_TILES)
-        load_row_tiles(nc, q_sb, q, NODE_TILES)
+        load_row_tiles(wv_sb, wv, FEAT_TILES)
+        load_row_tiles(h_sb, h, NODE_TILES)
+        load_row_tiles(k_sb, k, NODE_TILES)
+        load_row_tiles(q_sb, q, NODE_TILES)
         for i in range(NODE_TILES):
             nc.sync.dma_start(out=prior_sb[:, i, :], in_=cooccur[i * P : (i + 1) * P, :])
 
@@ -82,78 +64,125 @@ def tile_semanticgraph_pb_kernel(tc, q, k, h, cooccur, wv, bv, out):
         make_identity(nc, ident_f32[:])
         ident_bf16 = const.tile([P, P], BF16)
         make_identity(nc, ident_bf16[:])
+        ones = const.tile([P, P], BF16)
+        nc.vector.memset(ones[:], 1.0)
         warm = const.tile([P, 1], F32)
         nc.vector.memset(warm[:], 0.0)
         nc.scalar.activation(out=warm[:], in_=warm[:], func=ACT.Exp)
 
-        wv_grouped = keep.tile([P, PACK * FEATS], BF16, align_bytes=64)
-        wv_codes = keep.tile([P, FEATS], U32, align_bytes=64)
-        wv_scales = keep.tile([P, FEATS], U8, align_bytes=64)
-        quantise_along_features(nc, psum_sc, ident_f32, wv_sb, FEAT_TILES, wv_grouped, wv_codes, wv_scales)
-        h_grouped = keep.tile([P, PACK * NODES], BF16, align_bytes=64)
-        h_codes = keep.tile([P, NODES], U32, align_bytes=64)
-        h_scales = keep.tile([P, NODES], U8, align_bytes=64)
-        quantise_along_features(nc, psum_sc, ident_f32, h_sb, NODE_TILES, h_grouped, h_codes, h_scales)
+        def feature_operand(rows_sb, n_rows, name):
+            return {
+                "rows": rows_sb,
+                "grouped": keep.tile([P, PACK * n_rows], BF16, align_bytes=64, name=name + "_grouped"),
+                "codes": keep.tile([P, n_rows], U32, align_bytes=64, name=name + "_codes"),
+                "scales": keep.tile([P, n_rows], U8, align_bytes=64, name=name + "_scales"),
+            }
+
+        def flip_pair(operand, pair):
+            flipped = psum_sc.tile([P, 2, 2, P], F32, tag="sc")
+            for j in range(2):
+                words = operand["rows"][:, 2 * pair + j, :].bitcast(F32)
+                for u in range(2):
+                    nc.tensor.transpose(flipped[:, j, u, :], words[:, u * P : (u + 1) * P], ident_f32[:])
+            first_word = 2 * (2 * pair * P)
+            nc.scalar.copy(
+                out=operand["grouped"][:]
+                .bitcast(F32)[:, first_word : first_word + 4 * P]
+                .rearrange("p (j n u) -> p j n u", j=2, u=2),
+                in_=flipped[:].rearrange("p j u n -> p j n u"),
+            )
+
+        def quantise_pair(operand, pair):
+            first = 2 * pair * P
+            nc.vector.quantize_mx(
+                out=operand["codes"][:, first : first + 2 * P].bitcast(FP8X4),
+                scales=operand["scales"][:, first : first + 2 * P],
+                in_=operand["grouped"][:, PACK * first : PACK * (first + 2 * P)],
+            )
+
+        wv_mx = feature_operand(wv_sb, FEATS, "wv")
+        h_mx = feature_operand(h_sb, NODES, "h")
+        k_mx = feature_operand(k_sb, NODES, "k")
+        q_mx = feature_operand(q_sb, NODES, "q")
+
+        for pair in range(FEAT_TILES // 2):
+            flip_pair(wv_mx, pair)
+            quantise_pair(wv_mx, pair)
+
+        bias_bank = psum_acc.tile([P, FEATS], F32, tag="acc")
+        nc.tensor.matmul(out=bias_bank[:], lhsT=ones[:], rhs=bias_row[:], start=True, stop=True)
+        bias_sb = const.tile([P, FEATS], BF16)
+        nc.scalar.copy(out=bias_sb[:], in_=bias_bank[:])
+
+        for pair in range(NODE_TILES // 2):
+            flip_pair(h_mx, pair)
+            quantise_pair(h_mx, pair)
 
         v_grouped = keep.tile([P, KEY_PASSES, FEATS, PACK], BF16, align_bytes=64)
         v_codes = keep.tile([P, KEY_PASSES, FEATS], U32, align_bytes=64)
         v_scales = keep.tile([P, KEY_PASSES, FEATS], U8, align_bytes=64)
-        for g in range(KEY_PASSES):
-            for c in range(FEAT_TILES):
-                feats = slice(c * P, (c + 1) * P)
-                v_bank = psum_acc.tile([P, PACK, P], F32, tag="acc")
-                for t in range(PACK):
-                    nodes = slice((PACK * g + t) * P, (PACK * g + t + 1) * P)
-                    nc.tensor.matmul_mx(
-                        out=v_bank[:, t, :],
-                        lhsT=h_codes[:, nodes].bitcast(FP8X4),
-                        lhsT_scale=h_scales[:, nodes],
-                        rhs=wv_codes[:, feats].bitcast(FP8X4),
-                        rhs_scale=wv_scales[:, feats],
-                        start=True,
-                        stop=True,
-                    )
-                nc.vector.tensor_tensor(
-                    out=v_grouped[:, g, feats, :],
-                    in0=v_bank[:].rearrange("p t f -> p f t"),
-                    in1=bias_sb[:, feats].unsqueeze(2).to_broadcast([P, P, PACK]),
-                    op=ALU.add,
+
+        def value_bank(g, c):
+            feats = slice(c * P, (c + 1) * P)
+            v_bank = psum_acc.tile([P, PACK, P], F32, tag="acc")
+            for t in range(PACK):
+                nodes = slice((PACK * g + t) * P, (PACK * g + t + 1) * P)
+                nc.tensor.matmul_mx(
+                    out=v_bank[:, t, :],
+                    lhsT=h_mx["codes"][:, nodes].bitcast(FP8X4),
+                    lhsT_scale=h_mx["scales"][:, nodes],
+                    rhs=wv_mx["codes"][:, feats].bitcast(FP8X4),
+                    rhs_scale=wv_mx["scales"][:, feats],
+                    start=True,
+                    stop=True,
                 )
-            nc.vector.quantize_mx(
-                out=v_codes[:, g, :].bitcast(FP8X4),
-                scales=v_scales[:, g, :],
-                in_=v_grouped[:, g, :, :].rearrange("p f t -> p (f t)"),
+            nc.vector.tensor_tensor(
+                out=v_grouped[:, g, feats, :],
+                in0=v_bank[:].rearrange("p t f -> p f t"),
+                in1=bias_sb[:, feats].unsqueeze(2).to_broadcast([P, P, PACK]),
+                op=ALU.add,
             )
 
-        k_grouped = keep.tile([P, PACK * NODES], BF16, align_bytes=64)
-        k_codes = keep.tile([P, NODES], U32, align_bytes=64)
-        k_scales = keep.tile([P, NODES], U8, align_bytes=64)
-        quantise_along_features(nc, psum_sc, ident_f32, k_sb, NODE_TILES, k_grouped, k_codes, k_scales)
-        q_grouped = keep.tile([P, PACK * NODES], BF16, align_bytes=64)
-        q_codes = keep.tile([P, NODES], U32, align_bytes=64)
-        q_scales = keep.tile([P, NODES], U8, align_bytes=64)
-        quantise_along_features(nc, psum_sc, ident_f32, q_sb, NODE_TILES, q_grouped, q_codes, q_scales)
+        pairs = [(k_mx, pair) for pair in range(NODE_TILES // 2)] + [(q_mx, pair) for pair in range(NODE_TILES // 2)]
+        for n in range(KEY_PASSES * FEAT_TILES):
+            g, c = divmod(n, FEAT_TILES)
+            value_bank(g, c)
+            flip_pair(pairs[n][0], pairs[n][1])
+            if n > 0:
+                quantise_pair(pairs[n - 1][0], pairs[n - 1][1])
+            if c == FEAT_TILES - 1:
+                nc.vector.quantize_mx(
+                    out=v_codes[:, g, :].bitcast(FP8X4),
+                    scales=v_scales[:, g, :],
+                    in_=v_grouped[:, g, :, :].rearrange("p f t -> p (f t)"),
+                )
+        quantise_pair(pairs[-1][0], pairs[-1][1])
 
-        for i in range(NODE_TILES):
+        tiles = [{} for i in range(NODE_TILES)]
+
+        def scores(i):
             queries = slice(i * P, (i + 1) * P)
-
-            score_banks = []
-            row_max = work.tile([P, KEY_PASSES], F32)
+            tiles[i]["score"] = []
             for g in range(KEY_PASSES):
                 keys = slice(g * K_PASS, (g + 1) * K_PASS)
                 score = psum_sc.tile([P, K_PASS], F32, tag="sc")
                 nc.tensor.matmul_mx(
                     out=score[:],
-                    lhsT=q_codes[:, queries].bitcast(FP8X4),
-                    lhsT_scale=q_scales[:, queries],
-                    rhs=k_codes[:, keys].bitcast(FP8X4),
-                    rhs_scale=k_scales[:, keys],
+                    lhsT=q_mx["codes"][:, queries].bitcast(FP8X4),
+                    lhsT_scale=q_mx["scales"][:, queries],
+                    rhs=k_mx["codes"][:, keys].bitcast(FP8X4),
+                    rhs_scale=k_mx["scales"][:, keys],
                     start=True,
                     stop=True,
                 )
-                nc.vector.tensor_reduce(out=row_max[:, g : g + 1], in_=score[:], axis=AXIS.X, op=ALU.max)
-                score_banks.append(score)
+                tiles[i]["score"].append(score)
 
+        def exponentials(i):
+            row_max = work.tile([P, KEY_PASSES], F32)
+            for g in range(KEY_PASSES):
+                nc.vector.tensor_reduce(
+                    out=row_max[:, g : g + 1], in_=tiles[i]["score"][g][:], axis=AXIS.X, op=ALU.max
+                )
             shift = work.tile([P, 1], F32)
             nc.vector.tensor_scalar(
                 out=shift[:],
@@ -168,27 +197,28 @@ def tile_semanticgraph_pb_kernel(tc, q, k, h, cooccur, wv, bv, out):
             for g in range(KEY_PASSES):
                 nc.scalar.activation(
                     out=expo[:, g * K_PASS : (g + 1) * K_PASS],
-                    in_=score_banks[g][:],
+                    in_=tiles[i]["score"][g][:],
                     func=ACT.Exp,
                     bias=shift[:],
                     scale=SCORE_SCALE,
                     accum_out=row_sum[:, g : g + 1],
                 )
+            tiles[i]["expo"] = expo
+            tiles[i]["row_sum"] = row_sum
+
+        def attention(i):
+            row_sum = tiles[i]["row_sum"]
             total = work.tile([P, 1], F32)
             nc.vector.tensor_tensor(out=total[:], in0=row_sum[:, 0:1], in1=row_sum[:, 1:2], op=ALU.add)
             inverse = work.tile([P, 1], F32)
             nc.vector.reciprocal(out=inverse[:], in_=total[:])
-
             att = work.tile([P, NODES], BF16)
             att_grouped = work.tile([P, KEY_PASSES, P, PACK], BF16, align_bytes=64)
-            att_codes = work.tile([P, KEY_PASSES, P], U32, align_bytes=64)
-            att_scales = work.tile([P, KEY_PASSES, P], U8, align_bytes=64)
-            result = psum_acc.tile([P, FEATS], F32, tag="acc")
             for g in range(KEY_PASSES):
                 keys = slice(g * K_PASS, (g + 1) * K_PASS)
                 nc.vector.scalar_tensor_tensor(
                     out=att[:, keys],
-                    in0=expo[:, keys],
+                    in0=tiles[i]["expo"][:, keys],
                     scalar=inverse[:],
                     in1=prior_sb[:, i, keys],
                     op0=ALU.mult,
@@ -199,10 +229,17 @@ def tile_semanticgraph_pb_kernel(tc, q, k, h, cooccur, wv, bv, out):
                     first = g * K_PASS + t * P
                     nc.tensor.transpose(att_flipped[:, t, :], att[:, first : first + P], ident_bf16[:])
                 nc.scalar.copy(out=att_grouped[:, g, :, :], in_=att_flipped[:].rearrange("p t r -> p r t"))
+            tiles[i]["att_grouped"] = att_grouped
+
+        def weighted_values(i):
+            att_codes = work.tile([P, KEY_PASSES, P], U32, align_bytes=64)
+            att_scales = work.tile([P, KEY_PASSES, P], U8, align_bytes=64)
+            result = psum_acc.tile([P, FEATS], F32, tag="acc")
+            for g in range(KEY_PASSES):
                 nc.vector.quantize_mx(
                     out=att_codes[:, g, :].bitcast(FP8X4),
                     scales=att_scales[:, g, :],
-                    in_=att_grouped[:, g, :, :].rearrange("p r t -> p (r t)"),
+                    in_=tiles[i]["att_grouped"][:, g, :, :].rearrange("p r t -> p (r t)"),
                 )
                 nc.tensor.matmul_mx(
                     out=result[:],
@@ -213,14 +250,29 @@ def tile_semanticgraph_pb_kernel(tc, q, k, h, cooccur, wv, bv, out):
                     start=(g == 0),
                     stop=(g == KEY_PASSES - 1),
                 )
+            tiles[i]["result"] = result
 
+        def residual(i):
             out_sb = work.tile([P, FEATS], F32)
             nc.vector.scalar_tensor_tensor(
                 out=out_sb[:],
-                in0=result[:],
+                in0=tiles[i]["result"][:],
                 scalar=0.0,
                 in1=h_sb[:, i, :],
                 op0=ALU.max,
                 op1=ALU.add,
             )
-            nc.sync.dma_start(out=out[queries, :], in_=out_sb[:])
+            nc.sync.dma_start(out=out[i * P : (i + 1) * P, :], in_=out_sb[:])
+
+        scores(0)
+        for s in range(NODE_TILES + 2):
+            if s + 1 < NODE_TILES:
+                scores(s + 1)
+            if s < NODE_TILES:
+                exponentials(s)
+            if s >= 2:
+                weighted_values(s - 2)
+            if 1 <= s <= NODE_TILES:
+                attention(s - 1)
+            if s >= 2:
+                residual(s - 2)

@@ -176,13 +176,15 @@ def tile_semanticgraph_pb_kernel(tc, q, k, h, cooccur, wv, bv, out):
                     stop=True,
                 )
                 tiles[i]["score"].append(score)
+            tiles[i]["row_max"] = work.tile([P, KEY_PASSES], F32, name="row_max")
+
+        def half_maximum(i, g):
+            nc.vector.tensor_reduce(
+                out=tiles[i]["row_max"][:, g : g + 1], in_=tiles[i]["score"][g][:], axis=AXIS.X, op=ALU.max
+            )
 
         def exponentials(i):
-            row_max = work.tile([P, KEY_PASSES], F32)
-            for g in range(KEY_PASSES):
-                nc.vector.tensor_reduce(
-                    out=row_max[:, g : g + 1], in_=tiles[i]["score"][g][:], axis=AXIS.X, op=ALU.max
-                )
+            row_max = tiles[i]["row_max"]
             shift = work.tile([P, 1], F32)
             nc.vector.tensor_scalar(
                 out=shift[:],
@@ -206,41 +208,49 @@ def tile_semanticgraph_pb_kernel(tc, q, k, h, cooccur, wv, bv, out):
             tiles[i]["expo"] = expo
             tiles[i]["row_sum"] = row_sum
 
-        def attention(i):
-            row_sum = tiles[i]["row_sum"]
+        def sum_of_halves(i):
             total = work.tile([P, 1], F32)
+            row_sum = tiles[i]["row_sum"]
             nc.vector.tensor_tensor(out=total[:], in0=row_sum[:, 0:1], in1=row_sum[:, 1:2], op=ALU.add)
+            tiles[i]["total"] = total
+
+        def inverse_of_sum(i):
             inverse = work.tile([P, 1], F32)
-            nc.vector.reciprocal(out=inverse[:], in_=total[:])
+            nc.vector.reciprocal(out=inverse[:], in_=tiles[i]["total"][:])
+            tiles[i]["inverse"] = inverse
+
+        def attention(i):
             att = work.tile([P, NODES], BF16)
-            att_grouped = work.tile([P, KEY_PASSES, P, PACK], BF16, align_bytes=64)
+            nc.vector.scalar_tensor_tensor(
+                out=att[:],
+                in0=tiles[i]["expo"][:],
+                scalar=tiles[i]["inverse"][:],
+                in1=prior_sb[:, i, :],
+                op0=ALU.mult,
+                op1=ALU.add,
+            )
+            att_flipped = psum_tp.tile([P, KEY_PASSES, PACK, P], BF16, tag="tp")
             for g in range(KEY_PASSES):
-                keys = slice(g * K_PASS, (g + 1) * K_PASS)
-                nc.vector.scalar_tensor_tensor(
-                    out=att[:, keys],
-                    in0=tiles[i]["expo"][:, keys],
-                    scalar=inverse[:],
-                    in1=prior_sb[:, i, keys],
-                    op0=ALU.mult,
-                    op1=ALU.add,
-                )
-                att_flipped = psum_tp.tile([P, PACK, P], BF16, tag="tp")
                 for t in range(PACK):
-                    first = g * K_PASS + t * P
-                    nc.tensor.transpose(att_flipped[:, t, :], att[:, first : first + P], ident_bf16[:])
-                nc.scalar.copy(out=att_grouped[:, g, :, :], in_=att_flipped[:].rearrange("p t r -> p r t"))
+                    first = (g * PACK + t) * P
+                    nc.tensor.transpose(att_flipped[:, g, t, :], att[:, first : first + P], ident_bf16[:])
+            tiles[i]["att_flipped"] = att_flipped
+
+        def regroup(i):
+            att_grouped = work.tile([P, KEY_PASSES, P, PACK], BF16, align_bytes=64)
+            nc.scalar.copy(out=att_grouped[:], in_=tiles[i]["att_flipped"][:].rearrange("p g t r -> p g r t"))
             tiles[i]["att_grouped"] = att_grouped
 
         def weighted_values(i):
             att_codes = work.tile([P, KEY_PASSES, P], U32, align_bytes=64)
             att_scales = work.tile([P, KEY_PASSES, P], U8, align_bytes=64)
+            nc.vector.quantize_mx(
+                out=att_codes[:].rearrange("p g r -> p (g r)").bitcast(FP8X4),
+                scales=att_scales[:].rearrange("p g r -> p (g r)"),
+                in_=tiles[i]["att_grouped"][:].rearrange("p g r t -> p (g r t)"),
+            )
             result = psum_acc.tile([P, FEATS], F32, tag="acc")
             for g in range(KEY_PASSES):
-                nc.vector.quantize_mx(
-                    out=att_codes[:, g, :].bitcast(FP8X4),
-                    scales=att_scales[:, g, :],
-                    in_=tiles[i]["att_grouped"][:, g, :, :].rearrange("p r t -> p (r t)"),
-                )
                 nc.tensor.matmul_mx(
                     out=result[:],
                     lhsT=att_codes[:, g, :].bitcast(FP8X4),
@@ -264,15 +274,28 @@ def tile_semanticgraph_pb_kernel(tc, q, k, h, cooccur, wv, bv, out):
             )
             nc.sync.dma_start(out=out[i * P : (i + 1) * P, :], in_=out_sb[:])
 
+        def is_tile(i):
+            return 0 <= i < NODE_TILES
+
         scores(0)
-        for s in range(NODE_TILES + 2):
-            if s + 1 < NODE_TILES:
+        for s in range(NODE_TILES + 4):
+            if is_tile(s - 2):
+                regroup(s - 2)
+            if is_tile(s + 1):
                 scores(s + 1)
-            if s < NODE_TILES:
+            if is_tile(s - 3):
+                weighted_values(s - 3)
+            if is_tile(s):
+                half_maximum(s, 0)
+            if is_tile(s - 1):
+                sum_of_halves(s - 1)
+            if is_tile(s):
+                half_maximum(s, 1)
+            if is_tile(s - 1):
+                inverse_of_sum(s - 1)
+            if is_tile(s - 4):
+                residual(s - 4)
+            if is_tile(s):
                 exponentials(s)
-            if s >= 2:
-                weighted_values(s - 2)
-            if 1 <= s <= NODE_TILES:
+            if is_tile(s - 1):
                 attention(s - 1)
-            if s >= 2:
-                residual(s - 2)

@@ -33,6 +33,7 @@ def tile_semanticgraph_pb_kernel(tc, q, k, h, cooccur, wv, bv, out):
         const = ctx.enter_context(tc.tile_pool(name="const", bufs=1))
         keep = ctx.enter_context(tc.tile_pool(name="keep", bufs=1))
         work = ctx.enter_context(tc.tile_pool(name="work", bufs=3))
+        ahead = ctx.enter_context(tc.tile_pool(name="ahead", bufs=4))
         psum_sc = ctx.enter_context(tc.psum_pool(name="psum_sc", bufs=4))
         psum_tp = ctx.enter_context(tc.psum_pool(name="psum_tp", bufs=2))
         psum_acc = ctx.enter_context(tc.psum_pool(name="psum_acc", bufs=2))
@@ -194,8 +195,8 @@ def tile_semanticgraph_pb_kernel(tc, q, k, h, cooccur, wv, bv, out):
                 op0=ALU.max,
                 op1=ALU.mult,
             )
-            expo = work.tile([P, NODES], F32)
-            row_sum = work.tile([P, KEY_PASSES], F32)
+            expo = ahead.tile([P, NODES], F32)
+            row_sum = ahead.tile([P, KEY_PASSES], F32)
             for g in range(KEY_PASSES):
                 nc.scalar.activation(
                     out=expo[:, g * K_PASS : (g + 1) * K_PASS],
@@ -278,24 +279,24 @@ def tile_semanticgraph_pb_kernel(tc, q, k, h, cooccur, wv, bv, out):
             return 0 <= i < NODE_TILES
 
         scores(0)
-        for s in range(NODE_TILES + 4):
-            if is_tile(s - 2):
-                regroup(s - 2)
+        for s in range(NODE_TILES + 6):
             if is_tile(s + 1):
                 scores(s + 1)
             if is_tile(s - 3):
-                weighted_values(s - 3)
+                regroup(s - 3)
             if is_tile(s):
                 half_maximum(s, 0)
-            if is_tile(s - 1):
-                sum_of_halves(s - 1)
+            if is_tile(s - 2):
+                sum_of_halves(s - 2)
             if is_tile(s):
                 half_maximum(s, 1)
-            if is_tile(s - 1):
-                inverse_of_sum(s - 1)
+            if is_tile(s - 2):
+                inverse_of_sum(s - 2)
+            if is_tile(s - 6):
+                residual(s - 6)
             if is_tile(s - 4):
-                residual(s - 4)
+                weighted_values(s - 4)
             if is_tile(s):
                 exponentials(s)
-            if is_tile(s - 1):
-                attention(s - 1)
+            if is_tile(s - 2):
+                attention(s - 2)

@@ -23,6 +23,7 @@ NODE_TILES = NODES // P
 FEAT_TILES = FEATS // P
 KEY_PASSES = NODES // K_PASS
 SCORE_SCALE = 1.0 / math.sqrt(FEATS)
+LEAD = 2
 
 FLOPS = 2 * NODES * FEATS * FEATS + 2 * NODES * NODES * FEATS + 2 * NODES * NODES * FEATS
 
@@ -39,8 +40,8 @@ def tile_semanticgraph_pb_kernel(tc, q, k, h, cooccur, wv, bv, out):
         psum_acc = ctx.enter_context(tc.psum_pool(name="psum_acc", bufs=2))
         ctx.enter_context(tc.manual_schedule())
 
-        def load_row_tiles(rows_sb, rows, n_tiles):
-            for first in range(0, n_tiles, 2):
+        def load_row_tiles(rows_sb, rows, first_tile, n_tiles):
+            for first in range(first_tile, first_tile + n_tiles, 2):
                 nc.sync.dma_start(
                     out=rows_sb[:, first : first + 2, :],
                     in_=rows[first * P : (first + 2) * P, :].rearrange("(t p) f -> p t f", p=P),
@@ -54,10 +55,11 @@ def tile_semanticgraph_pb_kernel(tc, q, k, h, cooccur, wv, bv, out):
         k_sb = keep.tile([P, NODE_TILES, FEATS], BF16)
         q_sb = keep.tile([P, NODE_TILES, FEATS], BF16)
         prior_sb = keep.tile([P, NODE_TILES, NODES], BF16)
-        load_row_tiles(wv_sb, wv, FEAT_TILES)
-        load_row_tiles(h_sb, h, NODE_TILES)
-        load_row_tiles(k_sb, k, NODE_TILES)
-        load_row_tiles(q_sb, q, NODE_TILES)
+        load_row_tiles(h_sb, h, 0, PACK)
+        load_row_tiles(wv_sb, wv, 0, FEAT_TILES)
+        load_row_tiles(h_sb, h, PACK, NODE_TILES - PACK)
+        load_row_tiles(k_sb, k, 0, NODE_TILES)
+        load_row_tiles(q_sb, q, 0, NODE_TILES)
         for i in range(NODE_TILES):
             nc.sync.dma_start(out=prior_sb[:, i, :], in_=cooccur[i * P : (i + 1) * P, :])
 
@@ -106,18 +108,17 @@ def tile_semanticgraph_pb_kernel(tc, q, k, h, cooccur, wv, bv, out):
         k_mx = feature_operand(k_sb, NODES, "k")
         q_mx = feature_operand(q_sb, NODES, "q")
 
-        for pair in range(FEAT_TILES // 2):
-            flip_pair(wv_mx, pair)
-            quantise_pair(wv_mx, pair)
-
+        for pair in range(PACK // 2):
+            flip_pair(h_mx, pair)
+            quantise_pair(h_mx, pair)
+        flip_pair(wv_mx, 0)
+        quantise_pair(wv_mx, 0)
         bias_bank = psum_acc.tile([P, FEATS], F32, tag="acc")
         nc.tensor.matmul(out=bias_bank[:], lhsT=ones[:], rhs=bias_row[:], start=True, stop=True)
         bias_sb = const.tile([P, FEATS], BF16)
         nc.scalar.copy(out=bias_sb[:], in_=bias_bank[:])
-
-        for pair in range(NODE_TILES // 2):
-            flip_pair(h_mx, pair)
-            quantise_pair(h_mx, pair)
+        flip_pair(wv_mx, 1)
+        quantise_pair(wv_mx, 1)
 
         v_grouped = keep.tile([P, KEY_PASSES, FEATS, PACK], BF16, align_bytes=64)
         v_codes = keep.tile([P, KEY_PASSES, FEATS], U32, align_bytes=64)
@@ -144,20 +145,26 @@ def tile_semanticgraph_pb_kernel(tc, q, k, h, cooccur, wv, bv, out):
                 op=ALU.add,
             )
 
-        pairs = [(k_mx, pair) for pair in range(NODE_TILES // 2)] + [(q_mx, pair) for pair in range(NODE_TILES // 2)]
-        for n in range(KEY_PASSES * FEAT_TILES):
-            g, c = divmod(n, FEAT_TILES)
-            value_bank(g, c)
+        pairs = (
+            [(h_mx, pair) for pair in range(PACK // 2, NODE_TILES // 2)]
+            + [(k_mx, pair) for pair in range(NODE_TILES // 2)]
+            + [(q_mx, pair) for pair in range(NODE_TILES // 2)]
+        )
+        for n in range(LEAD):
             flip_pair(pairs[n][0], pairs[n][1])
-            if n > 0:
-                quantise_pair(pairs[n - 1][0], pairs[n - 1][1])
-            if c == FEAT_TILES - 1:
+        for n in range(len(pairs)):
+            g, c = divmod(n, FEAT_TILES)
+            if g < KEY_PASSES:
+                value_bank(g, c)
+            if n + LEAD < len(pairs):
+                flip_pair(pairs[n + LEAD][0], pairs[n + LEAD][1])
+            quantise_pair(pairs[n][0], pairs[n][1])
+            if g < KEY_PASSES and c == FEAT_TILES - 1:
                 nc.vector.quantize_mx(
                     out=v_codes[:, g, :].bitcast(FP8X4),
                     scales=v_scales[:, g, :],
                     in_=v_grouped[:, g, :, :].rearrange("p f t -> p (f t)"),
                 )
-        quantise_pair(pairs[-1][0], pairs[-1][1])
 
         tiles = [{} for i in range(NODE_TILES)]
 
@@ -238,7 +245,7 @@ def tile_semanticgraph_pb_kernel(tc, q, k, h, cooccur, wv, bv, out):
             tiles[i]["att_flipped"] = att_flipped
 
         def regroup(i):
-            att_grouped = work.tile([P, KEY_PASSES, P, PACK], BF16, align_bytes=64)
+            att_grouped = ahead.tile([P, KEY_PASSES, P, PACK], BF16, align_bytes=64)
             nc.scalar.copy(out=att_grouped[:], in_=tiles[i]["att_flipped"][:].rearrange("p g t r -> p g r t"))
             tiles[i]["att_grouped"] = att_grouped
 
@@ -279,24 +286,24 @@ def tile_semanticgraph_pb_kernel(tc, q, k, h, cooccur, wv, bv, out):
             return 0 <= i < NODE_TILES
 
         scores(0)
-        for s in range(NODE_TILES + 6):
+        for s in range(NODE_TILES + 7):
+            if is_tile(s - 2):
+                sum_of_halves(s - 2)
             if is_tile(s + 1):
                 scores(s + 1)
             if is_tile(s - 3):
                 regroup(s - 3)
+            if is_tile(s - 7):
+                residual(s - 7)
             if is_tile(s):
                 half_maximum(s, 0)
             if is_tile(s - 2):
-                sum_of_halves(s - 2)
+                inverse_of_sum(s - 2)
+            if is_tile(s - 5):
+                weighted_values(s - 5)
             if is_tile(s):
                 half_maximum(s, 1)
             if is_tile(s - 2):
-                inverse_of_sum(s - 2)
-            if is_tile(s - 6):
-                residual(s - 6)
-            if is_tile(s - 4):
-                weighted_values(s - 4)
+                attention(s - 2)
             if is_tile(s):
                 exponentials(s)
-            if is_tile(s - 2):
-                attention(s - 2)

@@ -34,10 +34,10 @@ def tile_semanticgraph_pb_kernel(tc, q, k, h, cooccur, wv, bv, out):
         const = ctx.enter_context(tc.tile_pool(name="const", bufs=1))
         keep = ctx.enter_context(tc.tile_pool(name="keep", bufs=1))
         work = ctx.enter_context(tc.tile_pool(name="work", bufs=3))
-        ahead = ctx.enter_context(tc.tile_pool(name="ahead", bufs=4))
+        ahead = ctx.enter_context(tc.tile_pool(name="ahead", bufs=5))
         psum_sc = ctx.enter_context(tc.psum_pool(name="psum_sc", bufs=4))
-        psum_tp = ctx.enter_context(tc.psum_pool(name="psum_tp", bufs=2))
-        psum_acc = ctx.enter_context(tc.psum_pool(name="psum_acc", bufs=2))
+        psum_tp = ctx.enter_context(tc.psum_pool(name="psum_tp", bufs=3))
+        psum_acc = ctx.enter_context(tc.psum_pool(name="psum_acc", bufs=1))
         ctx.enter_context(tc.manual_schedule())
 
         def load_row_tiles(rows_sb, rows, first_tile, n_tiles):
@@ -49,7 +49,7 @@ def tile_semanticgraph_pb_kernel(tc, q, k, h, cooccur, wv, bv, out):
 
         bias_row = const.tile([P, FEATS], BF16)
         nc.vector.memset(bias_row[:].bitcast(I32), 0)
-        nc.scalar.dma_start(out=bias_row[0:1, :], in_=bv.rearrange("(o f) -> o f", o=1))
+        nc.sync.dma_start(out=bias_row[0:1, :], in_=bv.rearrange("(o f) -> o f", o=1))
         wv_sb = keep.tile([P, FEAT_TILES, FEATS], BF16)
         h_sb = keep.tile([P, NODE_TILES, FEATS], BF16)
         k_sb = keep.tile([P, NODE_TILES, FEATS], BF16)
@@ -57,9 +57,10 @@ def tile_semanticgraph_pb_kernel(tc, q, k, h, cooccur, wv, bv, out):
         prior_sb = keep.tile([P, NODE_TILES, NODES], BF16)
         load_row_tiles(h_sb, h, 0, PACK)
         load_row_tiles(wv_sb, wv, 0, FEAT_TILES)
-        load_row_tiles(h_sb, h, PACK, NODE_TILES - PACK)
         load_row_tiles(k_sb, k, 0, NODE_TILES)
-        load_row_tiles(q_sb, q, 0, NODE_TILES)
+        load_row_tiles(q_sb, q, 0, PACK)
+        load_row_tiles(h_sb, h, PACK, NODE_TILES - PACK)
+        load_row_tiles(q_sb, q, PACK, NODE_TILES - PACK)
         for i in range(NODE_TILES):
             nc.sync.dma_start(out=prior_sb[:, i, :], in_=cooccur[i * P : (i + 1) * P, :])
 
@@ -81,8 +82,8 @@ def tile_semanticgraph_pb_kernel(tc, q, k, h, cooccur, wv, bv, out):
                 "scales": keep.tile([P, n_rows], U8, align_bytes=64, name=name + "_scales"),
             }
 
-        def flip_pair(operand, pair):
-            flipped = psum_sc.tile([P, 2, 2, P], F32, tag="sc")
+        def flip_pair(operand, pair, pool, tag):
+            flipped = pool.tile([P, 2, 2, P], F32, tag=tag)
             for j in range(2):
                 words = operand["rows"][:, 2 * pair + j, :].bitcast(F32)
                 for u in range(2):
@@ -108,16 +109,17 @@ def tile_semanticgraph_pb_kernel(tc, q, k, h, cooccur, wv, bv, out):
         k_mx = feature_operand(k_sb, NODES, "k")
         q_mx = feature_operand(q_sb, NODES, "q")
 
-        for pair in range(PACK // 2):
-            flip_pair(h_mx, pair)
-            quantise_pair(h_mx, pair)
-        flip_pair(wv_mx, 0)
-        quantise_pair(wv_mx, 0)
         bias_bank = psum_acc.tile([P, FEATS], F32, tag="acc")
         nc.tensor.matmul(out=bias_bank[:], lhsT=ones[:], rhs=bias_row[:], start=True, stop=True)
         bias_sb = const.tile([P, FEATS], BF16)
-        nc.scalar.copy(out=bias_sb[:], in_=bias_bank[:])
-        flip_pair(wv_mx, 1)
+        nc.vector.tensor_copy(out=bias_sb[:], in_=bias_bank[:])
+
+        for pair in range(PACK // 2):
+            flip_pair(h_mx, pair, psum_sc, "sc")
+            quantise_pair(h_mx, pair)
+        flip_pair(wv_mx, 0, psum_sc, "sc")
+        quantise_pair(wv_mx, 0)
+        flip_pair(wv_mx, 1, psum_sc, "sc")
         quantise_pair(wv_mx, 1)
 
         v_grouped = keep.tile([P, KEY_PASSES, FEATS, PACK], BF16, align_bytes=64)
@@ -126,7 +128,7 @@ def tile_semanticgraph_pb_kernel(tc, q, k, h, cooccur, wv, bv, out):
 
         def value_bank(g, c):
             feats = slice(c * P, (c + 1) * P)
-            v_bank = psum_acc.tile([P, PACK, P], F32, tag="acc")
+            v_bank = psum_tp.tile([P, PACK, P], F32, tag="tp")
             for t in range(PACK):
                 nodes = slice((PACK * g + t) * P, (PACK * g + t + 1) * P)
                 nc.tensor.matmul_mx(
@@ -145,26 +147,25 @@ def tile_semanticgraph_pb_kernel(tc, q, k, h, cooccur, wv, bv, out):
                 op=ALU.add,
             )
 
-        pairs = (
-            [(h_mx, pair) for pair in range(PACK // 2, NODE_TILES // 2)]
-            + [(k_mx, pair) for pair in range(NODE_TILES // 2)]
-            + [(q_mx, pair) for pair in range(NODE_TILES // 2)]
-        )
+        def quantise_values(g):
+            nc.vector.quantize_mx(
+                out=v_codes[:, g, :].bitcast(FP8X4),
+                scales=v_scales[:, g, :],
+                in_=v_grouped[:, g, :, :].rearrange("p f t -> p (f t)"),
+            )
+
+        first_pairs = [(k_mx, pair) for pair in range(NODE_TILES // 2)] + [(q_mx, 0)]
         for n in range(LEAD):
-            flip_pair(pairs[n][0], pairs[n][1])
-        for n in range(len(pairs)):
-            g, c = divmod(n, FEAT_TILES)
-            if g < KEY_PASSES:
-                value_bank(g, c)
-            if n + LEAD < len(pairs):
-                flip_pair(pairs[n + LEAD][0], pairs[n + LEAD][1])
-            quantise_pair(pairs[n][0], pairs[n][1])
-            if g < KEY_PASSES and c == FEAT_TILES - 1:
-                nc.vector.quantize_mx(
-                    out=v_codes[:, g, :].bitcast(FP8X4),
-                    scales=v_scales[:, g, :],
-                    in_=v_grouped[:, g, :, :].rearrange("p f t -> p (f t)"),
-                )
+            flip_pair(first_pairs[n][0], first_pairs[n][1], psum_sc, "sc")
+        for n in range(len(first_pairs)):
+            if n < FEAT_TILES:
+                value_bank(0, n)
+            if n + LEAD < len(first_pairs):
+                flip_pair(first_pairs[n + LEAD][0], first_pairs[n + LEAD][1], psum_sc, "sc")
+            quantise_pair(first_pairs[n][0], first_pairs[n][1])
+        flip_pair(q_mx, 1, psum_sc, "sc")
+        flip_pair(h_mx, 2, psum_sc, "sc")
+        flip_pair(h_mx, 3, psum_sc, "sc")
 
         tiles = [{} for i in range(NODE_TILES)]
 
@@ -191,7 +192,7 @@ def tile_semanticgraph_pb_kernel(tc, q, k, h, cooccur, wv, bv, out):
                 out=tiles[i]["row_max"][:, g : g + 1], in_=tiles[i]["score"][g][:], axis=AXIS.X, op=ALU.max
             )
 
-        def exponentials(i):
+        def shift_of(i):
             row_max = tiles[i]["row_max"]
             shift = work.tile([P, 1], F32)
             nc.vector.tensor_scalar(
@@ -202,6 +203,10 @@ def tile_semanticgraph_pb_kernel(tc, q, k, h, cooccur, wv, bv, out):
                 op0=ALU.max,
                 op1=ALU.mult,
             )
+            tiles[i]["shift"] = shift
+
+        def exponentials(i):
+            shift = tiles[i]["shift"]
             expo = ahead.tile([P, NODES], F32)
             row_sum = ahead.tile([P, KEY_PASSES], F32)
             for g in range(KEY_PASSES):
@@ -227,6 +232,18 @@ def tile_semanticgraph_pb_kernel(tc, q, k, h, cooccur, wv, bv, out):
             nc.vector.reciprocal(out=inverse[:], in_=tiles[i]["total"][:])
             tiles[i]["inverse"] = inverse
 
+        def normalise(i):
+            prob = ahead.tile([P, NODES], F32)
+            nc.gpsimd.tensor_scalar(
+                out=prob[:],
+                in0=tiles[i]["expo"][:],
+                scalar1=tiles[i]["inverse"][:],
+                scalar2=0.0,
+                op0=ALU.mult,
+                op1=ALU.add,
+            )
+            tiles[i]["prob"] = prob
+
         def attention(i):
             att = work.tile([P, NODES], BF16)
             nc.vector.scalar_tensor_tensor(
@@ -237,19 +254,49 @@ def tile_semanticgraph_pb_kernel(tc, q, k, h, cooccur, wv, bv, out):
                 op0=ALU.mult,
                 op1=ALU.add,
             )
+            tiles[i]["att"] = att
+
+        def flip_finished_attention(i):
             att_flipped = psum_tp.tile([P, KEY_PASSES, PACK, P], BF16, tag="tp")
             for g in range(KEY_PASSES):
                 for t in range(PACK):
                     first = (g * PACK + t) * P
-                    nc.tensor.transpose(att_flipped[:, g, t, :], att[:, first : first + P], ident_bf16[:])
-            tiles[i]["att_flipped"] = att_flipped
+                    nc.tensor.transpose(att_flipped[:, g, t, :], tiles[i]["att"][:, first : first + P], ident_bf16[:])
+            tiles[i]["att_halves"] = [att_flipped[:, g, :, :] for g in range(KEY_PASSES)]
+
+        def flip_attention(i):
+            prob = tiles[i]["prob"]
+            tiles[i]["att_halves"] = []
+            for g in range(KEY_PASSES):
+                half = psum_tp.tile([P, PACK, P], F32, tag="tp")
+                for t in range(PACK):
+                    first = (g * PACK + t) * P
+                    nc.tensor.matmul(
+                        out=half[:, t, :],
+                        lhsT=prior_sb[:, i, first : first + P],
+                        rhs=ident_bf16[:],
+                        start=True,
+                        stop=False,
+                    )
+                    nc.tensor.matmul(
+                        out=half[:, t, :],
+                        lhsT=prob[:, first : first + P],
+                        rhs=ident_f32[:],
+                        is_transpose=True,
+                        start=False,
+                        stop=True,
+                    )
+                tiles[i]["att_halves"].append(half[:])
 
         def regroup(i):
             att_grouped = ahead.tile([P, KEY_PASSES, P, PACK], BF16, align_bytes=64)
-            nc.scalar.copy(out=att_grouped[:], in_=tiles[i]["att_flipped"][:].rearrange("p g t r -> p g r t"))
+            for g in range(KEY_PASSES):
+                nc.scalar.copy(
+                    out=att_grouped[:, g, :, :], in_=tiles[i]["att_halves"][g].rearrange("p t r -> p r t")
+                )
             tiles[i]["att_grouped"] = att_grouped
 
-        def weighted_values(i):
+        def quantise_attention(i):
             att_codes = work.tile([P, KEY_PASSES, P], U32, align_bytes=64)
             att_scales = work.tile([P, KEY_PASSES, P], U8, align_bytes=64)
             nc.vector.quantize_mx(
@@ -257,7 +304,16 @@ def tile_semanticgraph_pb_kernel(tc, q, k, h, cooccur, wv, bv, out):
                 scales=att_scales[:].rearrange("p g r -> p (g r)"),
                 in_=tiles[i]["att_grouped"][:].rearrange("p g r t -> p (g r t)"),
             )
-            result = psum_acc.tile([P, FEATS], F32, tag="acc")
+            tiles[i]["att_codes"] = att_codes
+            tiles[i]["att_scales"] = att_scales
+
+        def weighted_values(i):
+            att_codes = tiles[i]["att_codes"]
+            att_scales = tiles[i]["att_scales"]
+            if i < NODE_TILES - 1:
+                result = psum_acc.tile([P, FEATS], F32, tag="acc")
+            else:
+                result = psum_sc.tile([P, FEATS], F32, tag="sc")
             for g in range(KEY_PASSES):
                 nc.tensor.matmul_mx(
                     out=result[:],
@@ -285,25 +341,60 @@ def tile_semanticgraph_pb_kernel(tc, q, k, h, cooccur, wv, bv, out):
         def is_tile(i):
             return 0 <= i < NODE_TILES
 
+        flips = {1: [(q_mx, 2)], 2: [(q_mx, 3)]}
+        quants = {0: [(h_mx, 2), (h_mx, 3)], 2: [(q_mx, 2)], 4: [(q_mx, 3)]}
+        banks = {1: [0, 1], 2: [2, 3]}
+
         scores(0)
-        for s in range(NODE_TILES + 7):
-            if is_tile(s - 2):
-                sum_of_halves(s - 2)
-            if is_tile(s + 1):
+        for s in range(NODE_TILES):
+            if s + 1 < NODE_TILES:
                 scores(s + 1)
-            if is_tile(s - 3):
-                regroup(s - 3)
-            if is_tile(s - 7):
-                residual(s - 7)
-            if is_tile(s):
-                half_maximum(s, 0)
-            if is_tile(s - 2):
-                inverse_of_sum(s - 2)
-            if is_tile(s - 5):
-                weighted_values(s - 5)
-            if is_tile(s):
-                half_maximum(s, 1)
-            if is_tile(s - 2):
-                attention(s - 2)
-            if is_tile(s):
-                exponentials(s)
+            half_maximum(s, 0)
+            half_maximum(s, 1)
+            if s == 0:
+                quantise_pair(q_mx, 1)
+            if s >= 1:
+                sum_of_halves(s - 1)
+            shift_of(s)
+            exponentials(s)
+            if s >= 1:
+                inverse_of_sum(s - 1)
+                normalise(s - 1)
+            for c in banks.get(s, []):
+                value_bank(1, c)
+            if s >= 2:
+                flip_attention(s - 2)
+            for operand, pair in flips.get(s, []):
+                flip_pair(operand, pair, psum_tp, "tp")
+            if s >= 2:
+                regroup(s - 2)
+            for operand, pair in quants.get(s, []):
+                quantise_pair(operand, pair)
+            if s == 0:
+                quantise_values(0)
+            if s == 3:
+                quantise_values(1)
+            if s >= 4:
+                residual(s - 4)
+            if s >= 3:
+                quantise_attention(s - 3)
+                weighted_values(s - 3)
+
+        last = NODE_TILES - 1
+        flip_attention(last - 1)
+        regroup(last - 1)
+        sum_of_halves(last)
+        inverse_of_sum(last)
+        attention(last)
+        flip_finished_attention(last)
+        regroup(last)
+        residual(last - 3)
+        quantise_attention(last - 2)
+        weighted_values(last - 2)
+        quantise_attention(last - 1)
+        residual(last - 2)
+        weighted_values(last - 1)
+        quantise_attention(last)
+        weighted_values(last)
+        residual(last - 1)
+        residual(last)

@@ -264,9 +264,8 @@ def tile_semanticgraph_pb_kernel(tc, q, k, h, cooccur, wv, bv, out):
                     nc.tensor.transpose(att_flipped[:, g, t, :], tiles[i]["att"][:, first : first + P], ident_bf16[:])
             tiles[i]["att_halves"] = [att_flipped[:, g, :, :] for g in range(KEY_PASSES)]
 
-        def flip_attention(i):
-            prob = tiles[i]["prob"]
-            tiles[i]["att_halves"] = []
+        def lay_prior(i):
+            tiles[i]["att_banks"] = []
             for g in range(KEY_PASSES):
                 half = psum_tp.tile([P, PACK, P], F32, tag="tp")
                 for t in range(PACK):
@@ -275,18 +274,24 @@ def tile_semanticgraph_pb_kernel(tc, q, k, h, cooccur, wv, bv, out):
                         out=half[:, t, :],
                         lhsT=prior_sb[:, i, first : first + P],
                         rhs=ident_bf16[:],
-                        start=True,
+                        start=(t == 0),
                         stop=False,
                     )
+                tiles[i]["att_banks"].append(half)
+
+        def flip_attention(i):
+            for g in range(KEY_PASSES):
+                for t in range(PACK):
+                    first = (g * PACK + t) * P
                     nc.tensor.matmul(
-                        out=half[:, t, :],
-                        lhsT=prob[:, first : first + P],
+                        out=tiles[i]["att_banks"][g][:, t, :],
+                        lhsT=tiles[i]["prob"][:, first : first + P],
                         rhs=ident_f32[:],
                         is_transpose=True,
                         start=False,
-                        stop=True,
+                        stop=(t == PACK - 1),
                     )
-                tiles[i]["att_halves"].append(half[:])
+            tiles[i]["att_halves"] = [bank[:] for bank in tiles[i]["att_banks"]]
 
         def regroup(i):
             att_grouped = ahead.tile([P, KEY_PASSES, P, PACK], BF16, align_bytes=64)
@@ -357,12 +362,10 @@ def tile_semanticgraph_pb_kernel(tc, q, k, h, cooccur, wv, bv, out):
                 sum_of_halves(s - 1)
             shift_of(s)
             exponentials(s)
-            if s >= 1:
-                inverse_of_sum(s - 1)
-                normalise(s - 1)
             for c in banks.get(s, []):
                 value_bank(1, c)
             if s >= 2:
+                lay_prior(s - 2)
                 flip_attention(s - 2)
             for operand, pair in flips.get(s, []):
                 flip_pair(operand, pair, psum_tp, "tp")
@@ -379,16 +382,20 @@ def tile_semanticgraph_pb_kernel(tc, q, k, h, cooccur, wv, bv, out):
             if s >= 3:
                 quantise_attention(s - 3)
                 weighted_values(s - 3)
+            if s >= 1:
+                inverse_of_sum(s - 1)
+                normalise(s - 1)
 
         last = NODE_TILES - 1
+        lay_prior(last - 1)
         flip_attention(last - 1)
         regroup(last - 1)
+        residual(last - 3)
         sum_of_halves(last)
         inverse_of_sum(last)
         attention(last)
         flip_finished_attention(last)
         regroup(last)
-        residual(last - 3)
         quantise_attention(last - 2)
         weighted_values(last - 2)
         quantise_attention(last - 1)

@@ -195,13 +195,15 @@ def tile_semanticgraph_pb_kernel(tc, q, k, h, cooccur, wv, bv, out):
         def shift_of(i):
             row_max = tiles[i]["row_max"]
             shift = work.tile([P, 1], F32)
+            scaled = work.tile([P, KEY_PASSES], F32)
             nc.vector.tensor_scalar(
-                out=shift[:],
-                in0=row_max[:, 0:1],
-                scalar1=row_max[:, 1:2],
-                scalar2=-SCORE_SCALE,
-                op0=ALU.max,
-                op1=ALU.mult,
+                out=scaled[:],
+                in0=row_max[:],
+                scalar1=-SCORE_SCALE,
+                scalar2=None,
+                op0=ALU.mult,
+                op1=ALU.min,
+                accum_out=shift[:],
             )
             tiles[i]["shift"] = shift
 
@@ -223,8 +225,7 @@ def tile_semanticgraph_pb_kernel(tc, q, k, h, cooccur, wv, bv, out):
 
         def sum_of_halves(i):
             total = work.tile([P, 1], F32)
-            row_sum = tiles[i]["row_sum"]
-            nc.vector.tensor_tensor(out=total[:], in0=row_sum[:, 0:1], in1=row_sum[:, 1:2], op=ALU.add)
+            nc.vector.tensor_reduce(out=total[:], in_=tiles[i]["row_sum"][:], axis=AXIS.X, op=ALU.add)
             tiles[i]["total"] = total
 
         def inverse_of_sum(i):

@@ -23,7 +23,7 @@ NODE_TILES = NODES // P
 FEAT_TILES = FEATS // P
 KEY_PASSES = NODES // K_PASS
 SCORE_SCALE = 1.0 / math.sqrt(FEATS)
-LEAD = 2
+PSUM_TILES = (0, 1, 2, 3, 4, 5, 6)
 
 FLOPS = 2 * NODES * FEATS * FEATS + 2 * NODES * NODES * FEATS + 2 * NODES * NODES * FEATS
 
@@ -34,7 +34,7 @@ def tile_semanticgraph_pb_kernel(tc, q, k, h, cooccur, wv, bv, out):
         const = ctx.enter_context(tc.tile_pool(name="const", bufs=1))
         keep = ctx.enter_context(tc.tile_pool(name="keep", bufs=1))
         work = ctx.enter_context(tc.tile_pool(name="work", bufs=3))
-        ahead = ctx.enter_context(tc.tile_pool(name="ahead", bufs=5))
+        ahead = ctx.enter_context(tc.tile_pool(name="ahead", bufs=8))
         psum_sc = ctx.enter_context(tc.psum_pool(name="psum_sc", bufs=4))
         psum_tp = ctx.enter_context(tc.psum_pool(name="psum_tp", bufs=3))
         psum_acc = ctx.enter_context(tc.psum_pool(name="psum_acc", bufs=1))
@@ -55,10 +55,11 @@ def tile_semanticgraph_pb_kernel(tc, q, k, h, cooccur, wv, bv, out):
         k_sb = keep.tile([P, NODE_TILES, FEATS], BF16)
         q_sb = keep.tile([P, NODE_TILES, FEATS], BF16)
         prior_sb = keep.tile([P, NODE_TILES, NODES], BF16)
+        load_row_tiles(k_sb, k, 0, NODE_TILES)
+        load_row_tiles(q_sb, q, 0, 2)
         load_row_tiles(h_sb, h, 0, PACK)
         load_row_tiles(wv_sb, wv, 0, FEAT_TILES)
-        load_row_tiles(k_sb, k, 0, NODE_TILES)
-        load_row_tiles(q_sb, q, 0, PACK)
+        load_row_tiles(q_sb, q, 2, 2)
         load_row_tiles(h_sb, h, PACK, NODE_TILES - PACK)
         load_row_tiles(q_sb, q, PACK, NODE_TILES - PACK)
         for i in range(NODE_TILES):
@@ -114,14 +115,6 @@ def tile_semanticgraph_pb_kernel(tc, q, k, h, cooccur, wv, bv, out):
         bias_sb = const.tile([P, FEATS], BF16)
         nc.vector.tensor_copy(out=bias_sb[:], in_=bias_bank[:])
 
-        for pair in range(PACK // 2):
-            flip_pair(h_mx, pair, psum_sc, "sc")
-            quantise_pair(h_mx, pair)
-        flip_pair(wv_mx, 0, psum_sc, "sc")
-        quantise_pair(wv_mx, 0)
-        flip_pair(wv_mx, 1, psum_sc, "sc")
-        quantise_pair(wv_mx, 1)
-
         v_grouped = keep.tile([P, KEY_PASSES, FEATS, PACK], BF16, align_bytes=64)
         v_codes = keep.tile([P, KEY_PASSES, FEATS], U32, align_bytes=64)
         v_scales = keep.tile([P, KEY_PASSES, FEATS], U8, align_bytes=64)
@@ -154,20 +147,28 @@ def tile_semanticgraph_pb_kernel(tc, q, k, h, cooccur, wv, bv, out):
                 in_=v_grouped[:, g, :, :].rearrange("p f t -> p (f t)"),
             )
 
-        first_pairs = [(k_mx, pair) for pair in range(NODE_TILES // 2)] + [(q_mx, 0)]
-        for n in range(LEAD):
-            flip_pair(first_pairs[n][0], first_pairs[n][1], psum_sc, "sc")
-        for n in range(len(first_pairs)):
-            if n < FEAT_TILES:
-                value_bank(0, n)
-            if n + LEAD < len(first_pairs):
-                flip_pair(first_pairs[n + LEAD][0], first_pairs[n + LEAD][1], psum_sc, "sc")
-            quantise_pair(first_pairs[n][0], first_pairs[n][1])
+        flip_pair(k_mx, 0, psum_sc, "sc")
+        flip_pair(k_mx, 1, psum_sc, "sc")
+        flip_pair(k_mx, 2, psum_sc, "sc")
+        quantise_pair(k_mx, 0)
+        flip_pair(k_mx, 3, psum_sc, "sc")
+        quantise_pair(k_mx, 1)
+        flip_pair(q_mx, 0, psum_sc, "sc")
+        quantise_pair(k_mx, 2)
+        flip_pair(h_mx, 0, psum_sc, "sc")
+        quantise_pair(k_mx, 3)
+        flip_pair(h_mx, 1, psum_sc, "sc")
+        quantise_pair(q_mx, 0)
+        flip_pair(wv_mx, 0, psum_sc, "sc")
+        flip_pair(wv_mx, 1, psum_sc, "sc")
+        quantise_pair(h_mx, 0)
+        quantise_pair(h_mx, 1)
         flip_pair(q_mx, 1, psum_sc, "sc")
-        flip_pair(h_mx, 2, psum_sc, "sc")
-        flip_pair(h_mx, 3, psum_sc, "sc")
 
         tiles = [{} for i in range(NODE_TILES)]
+
+        def adds_in_psum(i):
+            return i in PSUM_TILES
 
         def scores(i):
             queries = slice(i * P, (i + 1) * P)
@@ -263,7 +264,7 @@ def tile_semanticgraph_pb_kernel(tc, q, k, h, cooccur, wv, bv, out):
                 for t in range(PACK):
                     first = (g * PACK + t) * P
                     nc.tensor.transpose(att_flipped[:, g, t, :], tiles[i]["att"][:, first : first + P], ident_bf16[:])
-            tiles[i]["att_halves"] = [att_flipped[:, g, :, :] for g in range(KEY_PASSES)]
+            tiles[i]["att_flipped"] = att_flipped
 
         def lay_prior(i):
             tiles[i]["att_banks"] = []
@@ -292,14 +293,16 @@ def tile_semanticgraph_pb_kernel(tc, q, k, h, cooccur, wv, bv, out):
                         start=False,
                         stop=(t == PACK - 1),
                     )
-            tiles[i]["att_halves"] = [bank[:] for bank in tiles[i]["att_banks"]]
 
         def regroup(i):
             att_grouped = ahead.tile([P, KEY_PASSES, P, PACK], BF16, align_bytes=64)
-            for g in range(KEY_PASSES):
-                nc.scalar.copy(
-                    out=att_grouped[:, g, :, :], in_=tiles[i]["att_halves"][g].rearrange("p t r -> p r t")
-                )
+            if adds_in_psum(i):
+                for g in range(KEY_PASSES):
+                    nc.scalar.copy(
+                        out=att_grouped[:, g, :, :], in_=tiles[i]["att_banks"][g][:].rearrange("p t r -> p r t")
+                    )
+            else:
+                nc.scalar.copy(out=att_grouped[:], in_=tiles[i]["att_flipped"][:].rearrange("p g t r -> p g r t"))
             tiles[i]["att_grouped"] = att_grouped
 
         def quantise_attention(i):
@@ -316,7 +319,7 @@ def tile_semanticgraph_pb_kernel(tc, q, k, h, cooccur, wv, bv, out):
         def weighted_values(i):
             att_codes = tiles[i]["att_codes"]
             att_scales = tiles[i]["att_scales"]
-            if i < NODE_TILES - 1:
+            if i < NODE_TILES - 5:
                 result = psum_acc.tile([P, FEATS], F32, tag="acc")
             else:
                 result = psum_sc.tile([P, FEATS], F32, tag="sc")
@@ -333,7 +336,7 @@ def tile_semanticgraph_pb_kernel(tc, q, k, h, cooccur, wv, bv, out):
             tiles[i]["result"] = result
 
         def residual(i):
-            out_sb = work.tile([P, FEATS], F32)
+            out_sb = ahead.tile([P, FEATS], F32)
             nc.vector.scalar_tensor_tensor(
                 out=out_sb[:],
                 in0=tiles[i]["result"][:],
@@ -347,62 +350,76 @@ def tile_semanticgraph_pb_kernel(tc, q, k, h, cooccur, wv, bv, out):
         def is_tile(i):
             return 0 <= i < NODE_TILES
 
-        flips = {1: [(q_mx, 2)], 2: [(q_mx, 3)]}
-        quants = {0: [(h_mx, 2), (h_mx, 3)], 2: [(q_mx, 2)], 4: [(q_mx, 3)]}
-        banks = {1: [0, 1], 2: [2, 3]}
+
+        flips = {1: [(q_mx, 2), (h_mx, 2)], 2: [(h_mx, 3)], 3: [(q_mx, 3)]}
+        quants = {0: [(wv_mx, 0), (wv_mx, 1), (q_mx, 1)], 2: [(q_mx, 2), (h_mx, 2)], 3: [(h_mx, 3)], 4: [(q_mx, 3)]}
+        banks = {1: [(0, 0), (0, 1)], 2: [(0, 2), (0, 3)], 3: [(1, 0), (1, 1)], 4: [(1, 2), (1, 3)]}
+        vquants = {3: [0], 5: [1]}
 
         scores(0)
-        for s in range(NODE_TILES):
-            if s + 1 < NODE_TILES:
+        for s in range(NODE_TILES + 0):
+            if is_tile(s + 1):
                 scores(s + 1)
-            half_maximum(s, 0)
-            half_maximum(s, 1)
-            if s == 0:
-                quantise_pair(q_mx, 1)
-            if s >= 1:
-                sum_of_halves(s - 1)
-            shift_of(s)
-            exponentials(s)
-            for c in banks.get(s, []):
-                value_bank(1, c)
-            if s >= 2:
-                lay_prior(s - 2)
-                flip_attention(s - 2)
             for operand, pair in flips.get(s, []):
                 flip_pair(operand, pair, psum_tp, "tp")
-            if s >= 2:
-                regroup(s - 2)
+            if is_tile(s - 0):
+                half_maximum(s - 0, 0)
+            if is_tile(s - 0):
+                half_maximum(s - 0, 1)
+            if is_tile(s - 5):
+                quantise_attention(s - 5)
+            if is_tile(s - 1):
+                sum_of_halves(s - 1)
+            if is_tile(s - 0):
+                shift_of(s - 0)
+            if is_tile(s - 0):
+                exponentials(s - 0)
             for operand, pair in quants.get(s, []):
                 quantise_pair(operand, pair)
-            if s == 0:
-                quantise_values(0)
-            if s == 3:
-                quantise_values(1)
-            if s >= 4:
-                residual(s - 4)
-            if s >= 3:
-                quantise_attention(s - 3)
-                weighted_values(s - 3)
-            if s >= 1:
+            for g in vquants.get(s, []):
+                quantise_values(g)
+            if is_tile(s - 1):
                 inverse_of_sum(s - 1)
+            if is_tile(s - 1) and adds_in_psum(s - 1):
                 normalise(s - 1)
+            if is_tile(s - 1) and not adds_in_psum(s - 1):
+                attention(s - 1)
+            for g, c in banks.get(s, []):
+                value_bank(g, c)
+            if is_tile(s - 2):
+                if adds_in_psum(s - 2):
+                    lay_prior(s - 2)
+                    flip_attention(s - 2)
+                else:
+                    flip_finished_attention(s - 2)
+            if is_tile(s - 2):
+                regroup(s - 2)
+            if is_tile(s - 6):
+                residual(s - 6)
+            if is_tile(s - 5):
+                weighted_values(s - 5)
 
-        last = NODE_TILES - 1
-        lay_prior(last - 1)
-        flip_attention(last - 1)
-        regroup(last - 1)
-        residual(last - 3)
-        sum_of_halves(last)
-        inverse_of_sum(last)
-        attention(last)
-        flip_finished_attention(last)
-        regroup(last)
-        quantise_attention(last - 2)
-        weighted_values(last - 2)
-        quantise_attention(last - 1)
-        residual(last - 2)
-        weighted_values(last - 1)
-        quantise_attention(last)
-        weighted_values(last)
-        residual(last - 1)
-        residual(last)
+        quantise_attention(3)
+        lay_prior(6)
+        flip_attention(6)
+        regroup(6)
+        residual(2)
+        weighted_values(3)
+        sum_of_halves(7)
+        quantise_attention(4)
+        inverse_of_sum(7)
+        weighted_values(4)
+        attention(7)
+        flip_finished_attention(7)
+        regroup(7)
+        residual(3)
+        quantise_attention(5)
+        weighted_values(5)
+        residual(4)
+        quantise_attention(6)
+        weighted_values(6)
+        residual(5)
+        quantise_attention(7)
+        weighted_values(7)
+        residual(6)
+        residual(7)

@@ -55,8 +55,9 @@ def tile_semanticgraph_pb_kernel(tc, q, k, h, cooccur, wv, bv, out):
         k_sb = keep.tile([P, NODE_TILES, FEATS], BF16)
         q_sb = keep.tile([P, NODE_TILES, FEATS], BF16)
         prior_sb = keep.tile([P, NODE_TILES, NODES], BF16)
-        load_row_tiles(k_sb, k, 0, NODE_TILES)
+        load_row_tiles(k_sb, k, 0, 2)
         load_row_tiles(q_sb, q, 0, 2)
+        load_row_tiles(k_sb, k, 2, NODE_TILES - 2)
         load_row_tiles(h_sb, h, 0, PACK)
         load_row_tiles(wv_sb, wv, 0, FEAT_TILES)
         load_row_tiles(q_sb, q, 2, 2)
@@ -83,14 +84,14 @@ def tile_semanticgraph_pb_kernel(tc, q, k, h, cooccur, wv, bv, out):
                 "scales": keep.tile([P, n_rows], U8, align_bytes=64, name=name + "_scales"),
             }
 
-        def flip_pair(operand, pair, pool, tag):
+        def flip_pair(operand, pair, pool, tag, copy=nc.scalar.copy):
             flipped = pool.tile([P, 2, 2, P], F32, tag=tag)
             for j in range(2):
                 words = operand["rows"][:, 2 * pair + j, :].bitcast(F32)
                 for u in range(2):
                     nc.tensor.transpose(flipped[:, j, u, :], words[:, u * P : (u + 1) * P], ident_f32[:])
             first_word = 2 * (2 * pair * P)
-            nc.scalar.copy(
+            copy(
                 out=operand["grouped"][:]
                 .bitcast(F32)[:, first_word : first_word + 4 * P]
                 .rearrange("p (j n u) -> p j n u", j=2, u=2),
@@ -147,48 +148,30 @@ def tile_semanticgraph_pb_kernel(tc, q, k, h, cooccur, wv, bv, out):
                 in_=v_grouped[:, g, :, :].rearrange("p f t -> p (f t)"),
             )
 
-        flip_pair(k_mx, 0, psum_sc, "sc")
-        flip_pair(k_mx, 1, psum_sc, "sc")
-        flip_pair(k_mx, 2, psum_sc, "sc")
-        quantise_pair(k_mx, 0)
-        flip_pair(k_mx, 3, psum_sc, "sc")
-        quantise_pair(k_mx, 1)
-        flip_pair(q_mx, 0, psum_sc, "sc")
-        quantise_pair(k_mx, 2)
-        flip_pair(h_mx, 0, psum_sc, "sc")
-        quantise_pair(k_mx, 3)
-        flip_pair(h_mx, 1, psum_sc, "sc")
-        quantise_pair(q_mx, 0)
-        flip_pair(wv_mx, 0, psum_sc, "sc")
-        flip_pair(wv_mx, 1, psum_sc, "sc")
-        quantise_pair(h_mx, 0)
-        quantise_pair(h_mx, 1)
-        flip_pair(q_mx, 1, psum_sc, "sc")
-
         tiles = [{} for i in range(NODE_TILES)]
 
-        def adds_in_psum(i):
-            return i in PSUM_TILES
+        def score_half(i, g):
+            queries = slice(i * P, (i + 1) * P)
+            keys = slice(g * K_PASS, (g + 1) * K_PASS)
+            score = psum_sc.tile([P, K_PASS], F32, tag="sc")
+            nc.tensor.matmul_mx(
+                out=score[:],
+                lhsT=q_mx["codes"][:, queries].bitcast(FP8X4),
+                lhsT_scale=q_mx["scales"][:, queries],
+                rhs=k_mx["codes"][:, keys].bitcast(FP8X4),
+                rhs_scale=k_mx["scales"][:, keys],
+                start=True,
+                stop=True,
+            )
+            tiles[i].setdefault("score", []).append(score)
 
         def scores(i):
-            queries = slice(i * P, (i + 1) * P)
-            tiles[i]["score"] = []
             for g in range(KEY_PASSES):
-                keys = slice(g * K_PASS, (g + 1) * K_PASS)
-                score = psum_sc.tile([P, K_PASS], F32, tag="sc")
-                nc.tensor.matmul_mx(
-                    out=score[:],
-                    lhsT=q_mx["codes"][:, queries].bitcast(FP8X4),
-                    lhsT_scale=q_mx["scales"][:, queries],
-                    rhs=k_mx["codes"][:, keys].bitcast(FP8X4),
-                    rhs_scale=k_mx["scales"][:, keys],
-                    start=True,
-                    stop=True,
-                )
-                tiles[i]["score"].append(score)
-            tiles[i]["row_max"] = work.tile([P, KEY_PASSES], F32, name="row_max")
+                score_half(i, g)
 
         def half_maximum(i, g):
+            if g == 0:
+                tiles[i]["row_max"] = work.tile([P, KEY_PASSES], F32, name="row_max")
             nc.vector.tensor_reduce(
                 out=tiles[i]["row_max"][:, g : g + 1], in_=tiles[i]["score"][g][:], axis=AXIS.X, op=ALU.max
             )
@@ -246,25 +229,24 @@ def tile_semanticgraph_pb_kernel(tc, q, k, h, cooccur, wv, bv, out):
             )
             tiles[i]["prob"] = prob
 
-        def attention(i):
-            att = work.tile([P, NODES], BF16)
+        def attention_half(i, g):
+            keys = slice(g * K_PASS, (g + 1) * K_PASS)
+            att = ahead.tile([P, K_PASS], BF16)
             nc.vector.scalar_tensor_tensor(
                 out=att[:],
-                in0=tiles[i]["expo"][:],
+                in0=tiles[i]["expo"][:, keys],
                 scalar=tiles[i]["inverse"][:],
-                in1=prior_sb[:, i, :],
+                in1=prior_sb[:, i, keys],
                 op0=ALU.mult,
                 op1=ALU.add,
             )
-            tiles[i]["att"] = att
+            tiles[i].setdefault("att", []).append(att)
 
-        def flip_finished_attention(i):
-            att_flipped = psum_tp.tile([P, KEY_PASSES, PACK, P], BF16, tag="tp")
-            for g in range(KEY_PASSES):
-                for t in range(PACK):
-                    first = (g * PACK + t) * P
-                    nc.tensor.transpose(att_flipped[:, g, t, :], tiles[i]["att"][:, first : first + P], ident_bf16[:])
-            tiles[i]["att_flipped"] = att_flipped
+        def flip_finished_half(i, g):
+            bank = psum_tp.tile([P, PACK, P], BF16, tag="tp")
+            for t in range(PACK):
+                nc.tensor.transpose(bank[:, t, :], tiles[i]["att"][g][:, t * P : (t + 1) * P], ident_bf16[:])
+            tiles[i].setdefault("att_banks", []).append(bank)
 
         def lay_prior(i):
             tiles[i]["att_banks"] = []
@@ -294,46 +276,61 @@ def tile_semanticgraph_pb_kernel(tc, q, k, h, cooccur, wv, bv, out):
                         stop=(t == PACK - 1),
                     )
 
+        def regroup_half(i, g):
+            if g == 0:
+                tiles[i]["att_grouped"] = ahead.tile(
+                    [P, KEY_PASSES, P, PACK], BF16, align_bytes=64, name="att_grouped"
+                )
+            nc.scalar.copy(
+                out=tiles[i]["att_grouped"][:, g, :, :],
+                in_=tiles[i]["att_banks"][g][:].rearrange("p t r -> p r t"),
+            )
+
         def regroup(i):
-            att_grouped = ahead.tile([P, KEY_PASSES, P, PACK], BF16, align_bytes=64)
-            if adds_in_psum(i):
-                for g in range(KEY_PASSES):
-                    nc.scalar.copy(
-                        out=att_grouped[:, g, :, :], in_=tiles[i]["att_banks"][g][:].rearrange("p t r -> p r t")
-                    )
-            else:
-                nc.scalar.copy(out=att_grouped[:], in_=tiles[i]["att_flipped"][:].rearrange("p g t r -> p g r t"))
-            tiles[i]["att_grouped"] = att_grouped
+            for g in range(KEY_PASSES):
+                regroup_half(i, g)
+
+        def codes_tiles(i):
+            tiles[i]["att_codes"] = work.tile([P, KEY_PASSES, P], U32, align_bytes=64, name="att_codes")
+            tiles[i]["att_scales"] = work.tile([P, KEY_PASSES, P], U8, align_bytes=64, name="att_scales")
 
         def quantise_attention(i):
-            att_codes = work.tile([P, KEY_PASSES, P], U32, align_bytes=64)
-            att_scales = work.tile([P, KEY_PASSES, P], U8, align_bytes=64)
+            codes_tiles(i)
             nc.vector.quantize_mx(
-                out=att_codes[:].rearrange("p g r -> p (g r)").bitcast(FP8X4),
-                scales=att_scales[:].rearrange("p g r -> p (g r)"),
+                out=tiles[i]["att_codes"][:].rearrange("p g r -> p (g r)").bitcast(FP8X4),
+                scales=tiles[i]["att_scales"][:].rearrange("p g r -> p (g r)"),
                 in_=tiles[i]["att_grouped"][:].rearrange("p g r t -> p (g r t)"),
             )
-            tiles[i]["att_codes"] = att_codes
-            tiles[i]["att_scales"] = att_scales
+
+        def quantise_half(i, g):
+            if g == 0:
+                codes_tiles(i)
+            nc.vector.quantize_mx(
+                out=tiles[i]["att_codes"][:, g, :].bitcast(FP8X4),
+                scales=tiles[i]["att_scales"][:, g, :],
+                in_=tiles[i]["att_grouped"][:, g, :, :].rearrange("p r t -> p (r t)"),
+            )
+
+        def weighted_half(i, g):
+            if g == 0:
+                if i < 3:
+                    result = psum_acc.tile([P, FEATS], F32, tag="acc")
+                else:
+                    result = psum_sc.tile([P, FEATS], F32, tag="sc")
+                tiles[i]["result"] = result
+            nc.tensor.matmul_mx(
+                out=tiles[i]["result"][:],
+                lhsT=tiles[i]["att_codes"][:, g, :].bitcast(FP8X4),
+                lhsT_scale=tiles[i]["att_scales"][:, g, :],
+                rhs=v_codes[:, g, :].bitcast(FP8X4),
+                rhs_scale=v_scales[:, g, :],
+                start=(g == 0),
+                stop=(g == KEY_PASSES - 1),
+            )
 
         def weighted_values(i):
-            att_codes = tiles[i]["att_codes"]
-            att_scales = tiles[i]["att_scales"]
-            if i < NODE_TILES - 5:
-                result = psum_acc.tile([P, FEATS], F32, tag="acc")
-            else:
-                result = psum_sc.tile([P, FEATS], F32, tag="sc")
             for g in range(KEY_PASSES):
-                nc.tensor.matmul_mx(
-                    out=result[:],
-                    lhsT=att_codes[:, g, :].bitcast(FP8X4),
-                    lhsT_scale=att_scales[:, g, :],
-                    rhs=v_codes[:, g, :].bitcast(FP8X4),
-                    rhs_scale=v_scales[:, g, :],
-                    start=(g == 0),
-                    stop=(g == KEY_PASSES - 1),
-                )
-            tiles[i]["result"] = result
+                weighted_half(i, g)
 
         def residual(i):
             out_sb = ahead.tile([P, FEATS], F32)
@@ -351,75 +348,101 @@ def tile_semanticgraph_pb_kernel(tc, q, k, h, cooccur, wv, bv, out):
             return 0 <= i < NODE_TILES
 
 
+        flip_pair(k_mx, 0, psum_sc, "sc")
+        flip_pair(q_mx, 0, psum_sc, "sc")
+        flip_pair(k_mx, 1, psum_sc, "sc")
+        flip_pair(k_mx, 2, psum_sc, "sc")
+        quantise_pair(k_mx, 0)
+        flip_pair(k_mx, 3, psum_sc, "sc")
+        quantise_pair(q_mx, 0)
+        flip_pair(h_mx, 0, psum_tp, "tp")
+        quantise_pair(k_mx, 1)
+        flip_pair(h_mx, 1, psum_tp, "tp")
+        score_half(0, 0)
+        quantise_pair(k_mx, 2)
+        quantise_pair(k_mx, 3)
+        flip_pair(q_mx, 1, psum_tp, "tp")
+        score_half(0, 1)
+        half_maximum(0, 0)
+        quantise_pair(h_mx, 0)
+        half_maximum(0, 1)
+        quantise_pair(h_mx, 1)
+        flip_pair(wv_mx, 0, psum_tp, "tp")
+        flip_pair(wv_mx, 1, psum_tp, "tp")
+
         flips = {1: [(q_mx, 2), (h_mx, 2)], 2: [(h_mx, 3)], 3: [(q_mx, 3)]}
-        quants = {0: [(wv_mx, 0), (wv_mx, 1), (q_mx, 1)], 2: [(q_mx, 2), (h_mx, 2)], 3: [(h_mx, 3)], 4: [(q_mx, 3)]}
+        quants = {0: [(wv_mx, 0)], 2: [(h_mx, 2)]}
         banks = {1: [(0, 0), (0, 1)], 2: [(0, 2), (0, 3)], 3: [(1, 0), (1, 1)], 4: [(1, 2), (1, 3)]}
+        quants1 = {0: [(q_mx, 1)], 1: [(wv_mx, 1)], 2: [(q_mx, 2)], 3: [(h_mx, 3)], 4: [(q_mx, 3)]}
+        banks1 = {}
         vquants = {3: [0], 5: [1]}
 
-        scores(0)
         for s in range(NODE_TILES + 0):
-            if is_tile(s + 1):
-                scores(s + 1)
             for operand, pair in flips.get(s, []):
                 flip_pair(operand, pair, psum_tp, "tp")
-            if is_tile(s - 0):
+            if is_tile(s + 1):
+                scores(s + 1)
+            if 1 <= s < NODE_TILES:
                 half_maximum(s - 0, 0)
-            if is_tile(s - 0):
+            if 1 <= s < NODE_TILES:
                 half_maximum(s - 0, 1)
-            if is_tile(s - 5):
-                quantise_attention(s - 5)
+            for operand, pair in quants1.get(s, []):
+                quantise_pair(operand, pair)
             if is_tile(s - 1):
                 sum_of_halves(s - 1)
             if is_tile(s - 0):
                 shift_of(s - 0)
             if is_tile(s - 0):
                 exponentials(s - 0)
+            if is_tile(s - 5):
+                quantise_attention(s - 5)
+            if s == NODE_TILES - 1:
+                quantise_attention(s - 4)
             for operand, pair in quants.get(s, []):
                 quantise_pair(operand, pair)
             for g in vquants.get(s, []):
                 quantise_values(g)
             if is_tile(s - 1):
                 inverse_of_sum(s - 1)
-            if is_tile(s - 1) and adds_in_psum(s - 1):
+            if is_tile(s - 1):
                 normalise(s - 1)
-            if is_tile(s - 1) and not adds_in_psum(s - 1):
-                attention(s - 1)
+            if is_tile(s - 6):
+                residual(s - 6)
             for g, c in banks.get(s, []):
                 value_bank(g, c)
             if is_tile(s - 2):
-                if adds_in_psum(s - 2):
-                    lay_prior(s - 2)
-                    flip_attention(s - 2)
-                else:
-                    flip_finished_attention(s - 2)
+                lay_prior(s - 2)
+                flip_attention(s - 2)
             if is_tile(s - 2):
                 regroup(s - 2)
-            if is_tile(s - 6):
-                residual(s - 6)
             if is_tile(s - 5):
                 weighted_values(s - 5)
 
-        quantise_attention(3)
+        weighted_values(3)
         lay_prior(6)
         flip_attention(6)
         regroup(6)
-        residual(2)
-        weighted_values(3)
-        sum_of_halves(7)
         quantise_attention(4)
-        inverse_of_sum(7)
         weighted_values(4)
-        attention(7)
-        flip_finished_attention(7)
-        regroup(7)
+        residual(2)
+        sum_of_halves(7)
         residual(3)
+        inverse_of_sum(7)
         quantise_attention(5)
         weighted_values(5)
+        attention_half(7, 0)
+        attention_half(7, 1)
+        flip_finished_half(7, 0)
+        regroup_half(7, 0)
+        flip_finished_half(7, 1)
+        regroup_half(7, 1)
         residual(4)
         quantise_attention(6)
         weighted_values(6)
         residual(5)
-        quantise_attention(7)
-        weighted_values(7)
+        quantise_half(7, 0)
+        quantise_half(7, 1)
+        weighted_half(7, 0)
+        weighted_half(7, 1)
         residual(6)
         residual(7)

@@ -40,11 +40,11 @@ def tile_semanticgraph_pb_kernel(tc, q, k, h, cooccur, wv, bv, out):
         psum_acc = ctx.enter_context(tc.psum_pool(name="psum_acc", bufs=1))
         ctx.enter_context(tc.manual_schedule())
 
-        def load_row_tiles(rows_sb, rows, first_tile, n_tiles):
-            for first in range(first_tile, first_tile + n_tiles, 2):
+        def load_row_tiles(rows_sb, rows, first_tile, n_tiles, step=2):
+            for first in range(first_tile, first_tile + n_tiles, step):
                 nc.sync.dma_start(
-                    out=rows_sb[:, first : first + 2, :],
-                    in_=rows[first * P : (first + 2) * P, :].rearrange("(t p) f -> p t f", p=P),
+                    out=rows_sb[:, first : first + step, :],
+                    in_=rows[first * P : (first + step) * P, :].rearrange("(t p) f -> p t f", p=P),
                 )
 
         bias_row = const.tile([P, FEATS], BF16)
@@ -57,12 +57,12 @@ def tile_semanticgraph_pb_kernel(tc, q, k, h, cooccur, wv, bv, out):
         prior_sb = keep.tile([P, NODE_TILES, NODES], BF16)
         load_row_tiles(k_sb, k, 0, 2)
         load_row_tiles(q_sb, q, 0, 2)
-        load_row_tiles(k_sb, k, 2, NODE_TILES - 2)
-        load_row_tiles(h_sb, h, 0, PACK)
-        load_row_tiles(wv_sb, wv, 0, FEAT_TILES)
+        load_row_tiles(k_sb, k, 2, 6)
+        load_row_tiles(h_sb, h, 0, 4)
         load_row_tiles(q_sb, q, 2, 2)
-        load_row_tiles(h_sb, h, PACK, NODE_TILES - PACK)
-        load_row_tiles(q_sb, q, PACK, NODE_TILES - PACK)
+        load_row_tiles(wv_sb, wv, 0, 4)
+        load_row_tiles(h_sb, h, 4, 4)
+        load_row_tiles(q_sb, q, 4, 4)
         for i in range(NODE_TILES):
             nc.sync.dma_start(out=prior_sb[:, i, :], in_=cooccur[i * P : (i + 1) * P, :])
 
@@ -179,15 +179,13 @@ def tile_semanticgraph_pb_kernel(tc, q, k, h, cooccur, wv, bv, out):
         def shift_of(i):
             row_max = tiles[i]["row_max"]
             shift = work.tile([P, 1], F32)
-            scaled = work.tile([P, KEY_PASSES], F32)
             nc.vector.tensor_scalar(
-                out=scaled[:],
-                in0=row_max[:],
-                scalar1=-SCORE_SCALE,
-                scalar2=None,
-                op0=ALU.mult,
-                op1=ALU.min,
-                accum_out=shift[:],
+                out=shift[:],
+                in0=row_max[:, 0:1],
+                scalar1=row_max[:, 1:2],
+                scalar2=-SCORE_SCALE,
+                op0=ALU.max,
+                op1=ALU.mult,
             )
             tiles[i]["shift"] = shift
 
@@ -332,23 +330,26 @@ def tile_semanticgraph_pb_kernel(tc, q, k, h, cooccur, wv, bv, out):
             for g in range(KEY_PASSES):
                 weighted_half(i, g)
 
-        def residual(i):
-            out_sb = ahead.tile([P, FEATS], F32)
-            nc.vector.scalar_tensor_tensor(
-                out=out_sb[:],
-                in0=tiles[i]["result"][:],
-                scalar=0.0,
-                in1=h_sb[:, i, :],
-                op0=ALU.max,
-                op1=ALU.add,
-            )
-            nc.sync.dma_start(out=out[i * P : (i + 1) * P, :], in_=out_sb[:])
+        def residual(i, parts=1):
+            width = FEATS // parts
+            for part in range(parts):
+                feats = slice(part * width, (part + 1) * width)
+                out_sb = ahead.tile([P, FEATS], F32)
+                nc.vector.scalar_tensor_tensor(
+                    out=out_sb[:, feats],
+                    in0=tiles[i]["result"][:, feats],
+                    scalar=0.0,
+                    in1=h_sb[:, i, feats],
+                    op0=ALU.max,
+                    op1=ALU.add,
+                )
+                nc.sync.dma_start(out=out[i * P : (i + 1) * P, feats], in_=out_sb[:, feats])
 
         def is_tile(i):
             return 0 <= i < NODE_TILES
 
 
-        flip_pair(k_mx, 0, psum_sc, "sc")
+        flip_pair(k_mx, 0, psum_sc, "sc", nc.vector.tensor_copy)
         flip_pair(q_mx, 0, psum_sc, "sc")
         flip_pair(k_mx, 1, psum_sc, "sc")
         flip_pair(k_mx, 2, psum_sc, "sc")
@@ -388,6 +389,8 @@ def tile_semanticgraph_pb_kernel(tc, q, k, h, cooccur, wv, bv, out):
                 half_maximum(s - 0, 1)
             for operand, pair in quants1.get(s, []):
                 quantise_pair(operand, pair)
+            if is_tile(s - 6):
+                residual(s - 6)
             if is_tile(s - 1):
                 sum_of_halves(s - 1)
             if is_tile(s - 0):
@@ -406,8 +409,6 @@ def tile_semanticgraph_pb_kernel(tc, q, k, h, cooccur, wv, bv, out):
                 inverse_of_sum(s - 1)
             if is_tile(s - 1):
                 normalise(s - 1)
-            if is_tile(s - 6):
-                residual(s - 6)
             for g, c in banks.get(s, []):
                 value_bank(g, c)
             if is_tile(s - 2):
@@ -445,4 +446,4 @@ def tile_semanticgraph_pb_kernel(tc, q, k, h, cooccur, wv, bv, out):
         weighted_half(7, 0)
         weighted_half(7, 1)
         residual(6)
-        residual(7)
+        residual(7, 2)

@@ -49,13 +49,13 @@ def tile_semanticgraph_pb_kernel(tc, q, k, h, cooccur, wv, bv, out):
 
         bias_row = const.tile([P, FEATS], BF16)
         nc.vector.memset(bias_row[:].bitcast(I32), 0)
-        nc.sync.dma_start(out=bias_row[0:1, :], in_=bv.rearrange("(o f) -> o f", o=1))
         wv_sb = keep.tile([P, FEAT_TILES, FEATS], BF16)
         h_sb = keep.tile([P, NODE_TILES, FEATS], BF16)
         k_sb = keep.tile([P, NODE_TILES, FEATS], BF16)
         q_sb = keep.tile([P, NODE_TILES, FEATS], BF16)
         prior_sb = keep.tile([P, NODE_TILES, NODES], BF16)
         load_row_tiles(k_sb, k, 0, 2)
+        nc.sync.dma_start(out=bias_row[0:1, :], in_=bv.rearrange("(o f) -> o f", o=1))
         load_row_tiles(q_sb, q, 0, 2)
         load_row_tiles(k_sb, k, 2, 6)
         load_row_tiles(h_sb, h, 0, 4)
@@ -111,10 +111,12 @@ def tile_semanticgraph_pb_kernel(tc, q, k, h, cooccur, wv, bv, out):
         k_mx = feature_operand(k_sb, NODES, "k")
         q_mx = feature_operand(q_sb, NODES, "q")
 
-        bias_bank = psum_acc.tile([P, FEATS], F32, tag="acc")
-        nc.tensor.matmul(out=bias_bank[:], lhsT=ones[:], rhs=bias_row[:], start=True, stop=True)
         bias_sb = const.tile([P, FEATS], BF16)
-        nc.vector.tensor_copy(out=bias_sb[:], in_=bias_bank[:])
+
+        def spread_bias():
+            bias_bank = psum_acc.tile([P, FEATS], F32, tag="acc")
+            nc.tensor.matmul(out=bias_bank[:], lhsT=ones[:], rhs=bias_row[:], start=True, stop=True)
+            nc.vector.tensor_copy(out=bias_sb[:], in_=bias_bank[:])
 
         v_grouped = keep.tile([P, KEY_PASSES, FEATS, PACK], BF16, align_bytes=64)
         v_codes = keep.tile([P, KEY_PASSES, FEATS], U32, align_bytes=64)
@@ -350,6 +352,7 @@ def tile_semanticgraph_pb_kernel(tc, q, k, h, cooccur, wv, bv, out):
 
 
         flip_pair(k_mx, 0, psum_sc, "sc", nc.vector.tensor_copy)
+        spread_bias()
         flip_pair(q_mx, 0, psum_sc, "sc")
         flip_pair(k_mx, 1, psum_sc, "sc")
         flip_pair(k_mx, 2, psum_sc, "sc")

@@ -98,12 +98,13 @@ def tile_semanticgraph_pb_kernel(tc, q, k, h, cooccur, wv, bv, out):
                 in_=flipped[:].rearrange("p j u n -> p j n u"),
             )
 
-        def quantise_pair(operand, pair):
+        def quantise_pair(operand, pair, n_pairs=1):
             first = 2 * pair * P
+            end = first + 2 * n_pairs * P
             nc.vector.quantize_mx(
-                out=operand["codes"][:, first : first + 2 * P].bitcast(FP8X4),
-                scales=operand["scales"][:, first : first + 2 * P],
-                in_=operand["grouped"][:, PACK * first : PACK * (first + 2 * P)],
+                out=operand["codes"][:, first:end].bitcast(FP8X4),
+                scales=operand["scales"][:, first:end],
+                in_=operand["grouped"][:, PACK * first : PACK * end],
             )
 
         wv_mx = feature_operand(wv_sb, FEATS, "wv")
@@ -209,7 +210,8 @@ def tile_semanticgraph_pb_kernel(tc, q, k, h, cooccur, wv, bv, out):
 
         def sum_of_halves(i):
             total = work.tile([P, 1], F32)
-            nc.vector.tensor_reduce(out=total[:], in_=tiles[i]["row_sum"][:], axis=AXIS.X, op=ALU.add)
+            row_sum = tiles[i]["row_sum"]
+            nc.gpsimd.tensor_tensor(out=total[:], in0=row_sum[:, 0:1], in1=row_sum[:, 1:2], op=ALU.add)
             tiles[i]["total"] = total
 
         def inverse_of_sum(i):
@@ -219,14 +221,16 @@ def tile_semanticgraph_pb_kernel(tc, q, k, h, cooccur, wv, bv, out):
 
         def normalise(i):
             prob = ahead.tile([P, NODES], F32)
-            nc.gpsimd.tensor_scalar(
-                out=prob[:],
-                in0=tiles[i]["expo"][:],
-                scalar1=tiles[i]["inverse"][:],
-                scalar2=0.0,
-                op0=ALU.mult,
-                op1=ALU.add,
-            )
+            for g in range(KEY_PASSES):
+                keys = slice(g * K_PASS, (g + 1) * K_PASS)
+                nc.gpsimd.tensor_scalar(
+                    out=prob[:, keys],
+                    in0=tiles[i]["expo"][:, keys],
+                    scalar1=tiles[i]["inverse"][:],
+                    scalar2=0.0,
+                    op0=ALU.mult,
+                    op1=ALU.add,
+                )
             tiles[i]["prob"] = prob
 
         def attention_half(i, g):
@@ -248,33 +252,38 @@ def tile_semanticgraph_pb_kernel(tc, q, k, h, cooccur, wv, bv, out):
                 nc.tensor.transpose(bank[:, t, :], tiles[i]["att"][g][:, t * P : (t + 1) * P], ident_bf16[:])
             tiles[i].setdefault("att_banks", []).append(bank)
 
+        def lay_prior_half(i, g):
+            half = psum_tp.tile([P, PACK, P], F32, tag="tp")
+            for t in range(PACK):
+                first = (g * PACK + t) * P
+                nc.tensor.matmul(
+                    out=half[:, t, :],
+                    lhsT=prior_sb[:, i, first : first + P],
+                    rhs=ident_bf16[:],
+                    start=(t == 0),
+                    stop=False,
+                )
+            tiles[i].setdefault("att_banks", []).append(half)
+
+        def add_transposed_half(i, g):
+            for t in range(PACK):
+                first = (g * PACK + t) * P
+                nc.tensor.matmul(
+                    out=tiles[i]["att_banks"][g][:, t, :],
+                    lhsT=tiles[i]["prob"][:, first : first + P],
+                    rhs=ident_f32[:],
+                    is_transpose=True,
+                    start=False,
+                    stop=(t == PACK - 1),
+                )
+
         def lay_prior(i):
-            tiles[i]["att_banks"] = []
-            for g in range(KEY_PASSES):
-                half = psum_tp.tile([P, PACK, P], F32, tag="tp")
-                for t in range(PACK):
-                    first = (g * PACK + t) * P
-                    nc.tensor.matmul(
-                        out=half[:, t, :],
-                        lhsT=prior_sb[:, i, first : first + P],
-                        rhs=ident_bf16[:],
-                        start=(t == 0),
-                        stop=False,
-                    )
-                tiles[i]["att_banks"].append(half)
+            pass
 
         def flip_attention(i):
             for g in range(KEY_PASSES):
-                for t in range(PACK):
-                    first = (g * PACK + t) * P
-                    nc.tensor.matmul(
-                        out=tiles[i]["att_banks"][g][:, t, :],
-                        lhsT=tiles[i]["prob"][:, first : first + P],
-                        rhs=ident_f32[:],
-                        is_transpose=True,
-                        start=False,
-                        stop=(t == PACK - 1),
-                    )
+                lay_prior_half(i, g)
+                add_transposed_half(i, g)
 
         def regroup_half(i, g):
             if g == 0:
@@ -379,7 +388,8 @@ def tile_semanticgraph_pb_kernel(tc, q, k, h, cooccur, wv, bv, out):
         banks = {1: [(0, 0), (0, 1)], 2: [(0, 2), (0, 3)], 3: [(1, 0), (1, 1)], 4: [(1, 2), (1, 3)]}
         quants1 = {0: [(q_mx, 1)], 1: [(wv_mx, 1)], 2: [(q_mx, 2)], 3: [(h_mx, 3)], 4: [(q_mx, 3)]}
         banks1 = {}
-        vquants = {3: [0], 5: [1]}
+        vquants1 = {5: [1]}
+        vquants = {3: [0]}
 
         for s in range(NODE_TILES + 0):
             for operand, pair in flips.get(s, []):
@@ -390,8 +400,10 @@ def tile_semanticgraph_pb_kernel(tc, q, k, h, cooccur, wv, bv, out):
                 half_maximum(s - 0, 0)
             if 1 <= s < NODE_TILES:
                 half_maximum(s - 0, 1)
-            for operand, pair in quants1.get(s, []):
-                quantise_pair(operand, pair)
+            for job in quants1.get(s, []):
+                quantise_pair(*job)
+            for g in vquants1.get(s, []):
+                quantise_values(g)
             if is_tile(s - 6):
                 residual(s - 6)
             if is_tile(s - 1):
@@ -404,10 +416,12 @@ def tile_semanticgraph_pb_kernel(tc, q, k, h, cooccur, wv, bv, out):
                 quantise_attention(s - 5)
             if s == NODE_TILES - 1:
                 quantise_attention(s - 4)
-            for operand, pair in quants.get(s, []):
-                quantise_pair(operand, pair)
+            for job in quants.get(s, []):
+                quantise_pair(*job)
             for g in vquants.get(s, []):
                 quantise_values(g)
+            for g, c in banks1.get(s, []):
+                value_bank(g, c)
             if is_tile(s - 1):
                 inverse_of_sum(s - 1)
             if is_tile(s - 1):

from contextlib import ExitStack
import math

import concourse.mybir as mybir
from concourse.masks import make_identity

F32 = mybir.dt.float32
BF16 = mybir.dt.bfloat16
I32 = mybir.dt.int32
U32 = mybir.dt.uint32
U8 = mybir.dt.uint8
FP8X4 = mybir.dt.float8_e4m3fn_x4
ALU = mybir.AluOpType
ACT = mybir.ActivationFunctionType
AXIS = mybir.AxisListType

P = 128
PACK = 4
K_PASS = P * PACK
NODES = 1024
FEATS = 512
NODE_TILES = NODES // P
FEAT_TILES = FEATS // P
KEY_PASSES = NODES // K_PASS
SCORE_SCALE = 1.0 / math.sqrt(FEATS)
PSUM_TILES = (0, 1, 2, 3, 4, 5, 6)

FLOPS = 2 * NODES * FEATS * FEATS + 2 * NODES * NODES * FEATS + 2 * NODES * NODES * FEATS


def tile_semanticgraph_pb_kernel(tc, q, k, h, cooccur, wv, bv, out):
    nc = tc.nc
    with ExitStack() as ctx:
        const = ctx.enter_context(tc.tile_pool(name="const", bufs=1))
        keep = ctx.enter_context(tc.tile_pool(name="keep", bufs=1))
        work = ctx.enter_context(tc.tile_pool(name="work", bufs=3))
        ahead = ctx.enter_context(tc.tile_pool(name="ahead", bufs=8))
        psum_sc = ctx.enter_context(tc.psum_pool(name="psum_sc", bufs=4))
        psum_tp = ctx.enter_context(tc.psum_pool(name="psum_tp", bufs=3))
        psum_acc = ctx.enter_context(tc.psum_pool(name="psum_acc", bufs=1))
        ctx.enter_context(tc.manual_schedule())

        def load_row_tiles(rows_sb, rows, first_tile, n_tiles, step=2):
            for first in range(first_tile, first_tile + n_tiles, step):
                nc.sync.dma_start(
                    out=rows_sb[:, first : first + step, :],
                    in_=rows[first * P : (first + step) * P, :].rearrange("(t p) f -> p t f", p=P),
                )

        bias_row = const.tile([P, FEATS], BF16)
        nc.vector.memset(bias_row[:].bitcast(I32), 0)
        wv_sb = keep.tile([P, FEAT_TILES, FEATS], BF16)
        h_sb = keep.tile([P, NODE_TILES, FEATS], BF16)
        k_sb = keep.tile([P, NODE_TILES, FEATS], BF16)
        q_sb = keep.tile([P, NODE_TILES, FEATS], BF16)
        prior_sb = keep.tile([P, NODE_TILES, NODES], BF16)
        load_row_tiles(k_sb, k, 0, 2)
        nc.sync.dma_start(out=bias_row[0:1, :], in_=bv.rearrange("(o f) -> o f", o=1))
        load_row_tiles(q_sb, q, 0, 2)
        load_row_tiles(k_sb, k, 2, 6)
        load_row_tiles(h_sb, h, 0, 4)
        load_row_tiles(q_sb, q, 2, 2)
        load_row_tiles(wv_sb, wv, 0, 4)
        load_row_tiles(h_sb, h, 4, 4)
        load_row_tiles(q_sb, q, 4, 4)
        for i in range(NODE_TILES):
            nc.sync.dma_start(out=prior_sb[:, i, :], in_=cooccur[i * P : (i + 1) * P, :])

        ident_f32 = const.tile([P, P], F32)
        make_identity(nc, ident_f32[:])
        ident_bf16 = const.tile([P, P], BF16)
        make_identity(nc, ident_bf16[:])
        ones = const.tile([P, P], BF16)
        nc.vector.memset(ones[:], 1.0)
        warm = const.tile([P, 1], F32)
        nc.vector.memset(warm[:], 0.0)
        nc.scalar.activation(out=warm[:], in_=warm[:], func=ACT.Exp)

        def feature_operand(rows_sb, n_rows, name):
            return {
                "rows": rows_sb,
                "grouped": keep.tile([P, PACK * n_rows], BF16, align_bytes=64, name=name + "_grouped"),
                "codes": keep.tile([P, n_rows], U32, align_bytes=64, name=name + "_codes"),
                "scales": keep.tile([P, n_rows], U8, align_bytes=64, name=name + "_scales"),
            }

        def flip_pair(operand, pair, pool, tag, copy=nc.scalar.copy):
            flipped = pool.tile([P, 2, 2, P], F32, tag=tag)
            for j in range(2):
                words = operand["rows"][:, 2 * pair + j, :].bitcast(F32)
                for u in range(2):
                    nc.tensor.transpose(flipped[:, j, u, :], words[:, u * P : (u + 1) * P], ident_f32[:])
            first_word = 2 * (2 * pair * P)
            copy(
                out=operand["grouped"][:]
                .bitcast(F32)[:, first_word : first_word + 4 * P]
                .rearrange("p (j n u) -> p j n u", j=2, u=2),
                in_=flipped[:].rearrange("p j u n -> p j n u"),
            )

        def quantise_pair(operand, pair, n_pairs=1):
            first = 2 * pair * P
            end = first + 2 * n_pairs * P
            nc.vector.quantize_mx(
                out=operand["codes"][:, first:end].bitcast(FP8X4),
                scales=operand["scales"][:, first:end],
                in_=operand["grouped"][:, PACK * first : PACK * end],
            )

        wv_mx = feature_operand(wv_sb, FEATS, "wv")
        h_mx = feature_operand(h_sb, NODES, "h")
        k_mx = feature_operand(k_sb, NODES, "k")
        q_mx = feature_operand(q_sb, NODES, "q")

        bias_sb = const.tile([P, FEATS], BF16)

        def spread_bias():
            bias_bank = psum_acc.tile([P, FEATS], F32, tag="acc")
            nc.tensor.matmul(out=bias_bank[:], lhsT=ones[:], rhs=bias_row[:], start=True, stop=True)
            nc.vector.tensor_copy(out=bias_sb[:], in_=bias_bank[:])

        v_grouped = keep.tile([P, KEY_PASSES, FEATS, PACK], BF16, align_bytes=64)
        v_codes = keep.tile([P, KEY_PASSES, FEATS], U32, align_bytes=64)
        v_scales = keep.tile([P, KEY_PASSES, FEATS], U8, align_bytes=64)

        def value_bank(g, c):
            feats = slice(c * P, (c + 1) * P)
            v_bank = psum_tp.tile([P, PACK, P], F32, tag="tp")
            for t in range(PACK):
                nodes = slice((PACK * g + t) * P, (PACK * g + t + 1) * P)
                nc.tensor.matmul_mx(
                    out=v_bank[:, t, :],
                    lhsT=h_mx["codes"][:, nodes].bitcast(FP8X4),
                    lhsT_scale=h_mx["scales"][:, nodes],
                    rhs=wv_mx["codes"][:, feats].bitcast(FP8X4),
                    rhs_scale=wv_mx["scales"][:, feats],
                    start=True,
                    stop=True,
                )
            nc.vector.tensor_tensor(
                out=v_grouped[:, g, feats, :],
                in0=v_bank[:].rearrange("p t f -> p f t"),
                in1=bias_sb[:, feats].unsqueeze(2).to_broadcast([P, P, PACK]),
                op=ALU.add,
            )

        def quantise_values(g):
            nc.vector.quantize_mx(
                out=v_codes[:, g, :].bitcast(FP8X4),
                scales=v_scales[:, g, :],
                in_=v_grouped[:, g, :, :].rearrange("p f t -> p (f t)"),
            )

        tiles = [{} for i in range(NODE_TILES)]

        def score_half(i, g):
            queries = slice(i * P, (i + 1) * P)
            keys = slice(g * K_PASS, (g + 1) * K_PASS)
            score = psum_sc.tile([P, K_PASS], F32, tag="sc")
            nc.tensor.matmul_mx(
                out=score[:],
                lhsT=q_mx["codes"][:, queries].bitcast(FP8X4),
                lhsT_scale=q_mx["scales"][:, queries],
                rhs=k_mx["codes"][:, keys].bitcast(FP8X4),
                rhs_scale=k_mx["scales"][:, keys],
                start=True,
                stop=True,
            )
            tiles[i].setdefault("score", []).append(score)

        def scores(i):
            for g in range(KEY_PASSES):
                score_half(i, g)

        def half_maximum(i, g):
            if g == 0:
                tiles[i]["row_max"] = work.tile([P, KEY_PASSES], F32, name="row_max")
            nc.vector.tensor_reduce(
                out=tiles[i]["row_max"][:, g : g + 1], in_=tiles[i]["score"][g][:], axis=AXIS.X, op=ALU.max
            )

        def shift_of(i):
            row_max = tiles[i]["row_max"]
            shift = work.tile([P, 1], F32)
            nc.vector.tensor_scalar(
                out=shift[:],
                in0=row_max[:, 0:1],
                scalar1=row_max[:, 1:2],
                scalar2=-SCORE_SCALE,
                op0=ALU.max,
                op1=ALU.mult,
            )
            tiles[i]["shift"] = shift

        def exponentials(i):
            shift = tiles[i]["shift"]
            expo = ahead.tile([P, NODES], F32)
            row_sum = ahead.tile([P, KEY_PASSES], F32)
            for g in range(KEY_PASSES):
                nc.scalar.activation(
                    out=expo[:, g * K_PASS : (g + 1) * K_PASS],
                    in_=tiles[i]["score"][g][:],
                    func=ACT.Exp,
                    bias=shift[:],
                    scale=SCORE_SCALE,
                    accum_out=row_sum[:, g : g + 1],
                )
            tiles[i]["expo"] = expo
            tiles[i]["row_sum"] = row_sum

        def sum_of_halves(i):
            total = work.tile([P, 1], F32)
            row_sum = tiles[i]["row_sum"]
            nc.gpsimd.tensor_tensor(out=total[:], in0=row_sum[:, 0:1], in1=row_sum[:, 1:2], op=ALU.add)
            tiles[i]["total"] = total

        def inverse_of_sum(i):
            inverse = work.tile([P, 1], F32)
            nc.vector.reciprocal(out=inverse[:], in_=tiles[i]["total"][:])
            tiles[i]["inverse"] = inverse

        def normalise(i):
            prob = ahead.tile([P, NODES], F32)
            for g in range(KEY_PASSES):
                keys = slice(g * K_PASS, (g + 1) * K_PASS)
                nc.gpsimd.tensor_scalar(
                    out=prob[:, keys],
                    in0=tiles[i]["expo"][:, keys],
                    scalar1=tiles[i]["inverse"][:],
                    scalar2=0.0,
                    op0=ALU.mult,
                    op1=ALU.add,
                )
            tiles[i]["prob"] = prob

        def attention_half(i, g):
            keys = slice(g * K_PASS, (g + 1) * K_PASS)
            att = ahead.tile([P, K_PASS], BF16)
            nc.vector.scalar_tensor_tensor(
                out=att[:],
                in0=tiles[i]["expo"][:, keys],
                scalar=tiles[i]["inverse"][:],
                in1=prior_sb[:, i, keys],
                op0=ALU.mult,
                op1=ALU.add,
            )
            tiles[i].setdefault("att", []).append(att)

        def flip_finished_half(i, g):
            bank = psum_tp.tile([P, PACK, P], BF16, tag="tp")
            for t in range(PACK):
                nc.tensor.transpose(bank[:, t, :], tiles[i]["att"][g][:, t * P : (t + 1) * P], ident_bf16[:])
            tiles[i].setdefault("att_banks", []).append(bank)

        def lay_prior_half(i, g):
            half = psum_tp.tile([P, PACK, P], F32, tag="tp")
            for t in range(PACK):
                first = (g * PACK + t) * P
                nc.tensor.matmul(
                    out=half[:, t, :],
                    lhsT=prior_sb[:, i, first : first + P],
                    rhs=ident_bf16[:],
                    start=(t == 0),
                    stop=False,
                )
            tiles[i].setdefault("att_banks", []).append(half)

        def add_transposed_half(i, g):
            for t in range(PACK):
                first = (g * PACK + t) * P
                nc.tensor.matmul(
                    out=tiles[i]["att_banks"][g][:, t, :],
                    lhsT=tiles[i]["prob"][:, first : first + P],
                    rhs=ident_f32[:],
                    is_transpose=True,
                    start=False,
                    stop=(t == PACK - 1),
                )

        def lay_prior(i):
            pass

        def flip_attention(i):
            for g in range(KEY_PASSES):
                lay_prior_half(i, g)
                add_transposed_half(i, g)

        def regroup_half(i, g):
            if g == 0:
                tiles[i]["att_grouped"] = ahead.tile(
                    [P, KEY_PASSES, P, PACK], BF16, align_bytes=64, name="att_grouped"
                )
            nc.scalar.copy(
                out=tiles[i]["att_grouped"][:, g, :, :],
                in_=tiles[i]["att_banks"][g][:].rearrange("p t r -> p r t"),
            )

        def regroup(i):
            for g in range(KEY_PASSES):
                regroup_half(i, g)

        def codes_tiles(i):
            tiles[i]["att_codes"] = work.tile([P, KEY_PASSES, P], U32, align_bytes=64, name="att_codes")
            tiles[i]["att_scales"] = work.tile([P, KEY_PASSES, P], U8, align_bytes=64, name="att_scales")

        def quantise_attention(i):
            codes_tiles(i)
            nc.vector.quantize_mx(
                out=tiles[i]["att_codes"][:].rearrange("p g r -> p (g r)").bitcast(FP8X4),
                scales=tiles[i]["att_scales"][:].rearrange("p g r -> p (g r)"),
                in_=tiles[i]["att_grouped"][:].rearrange("p g r t -> p (g r t)"),
            )

        def quantise_half(i, g):
            if g == 0:
                codes_tiles(i)
            nc.vector.quantize_mx(
                out=tiles[i]["att_codes"][:, g, :].bitcast(FP8X4),
                scales=tiles[i]["att_scales"][:, g, :],
                in_=tiles[i]["att_grouped"][:, g, :, :].rearrange("p r t -> p (r t)"),
            )

        def weighted_half(i, g):
            if g == 0:
                if i < 3:
                    result = psum_acc.tile([P, FEATS], F32, tag="acc")
                else:
                    result = psum_sc.tile([P, FEATS], F32, tag="sc")
                tiles[i]["result"] = result
            nc.tensor.matmul_mx(
                out=tiles[i]["result"][:],
                lhsT=tiles[i]["att_codes"][:, g, :].bitcast(FP8X4),
                lhsT_scale=tiles[i]["att_scales"][:, g, :],
                rhs=v_codes[:, g, :].bitcast(FP8X4),
                rhs_scale=v_scales[:, g, :],
                start=(g == 0),
                stop=(g == KEY_PASSES - 1),
            )

        def weighted_values(i):
            for g in range(KEY_PASSES):
                weighted_half(i, g)

        def residual(i, parts=1):
            width = FEATS // parts
            for part in range(parts):
                feats = slice(part * width, (part + 1) * width)
                out_sb = ahead.tile([P, FEATS], F32)
                nc.vector.scalar_tensor_tensor(
                    out=out_sb[:, feats],
                    in0=tiles[i]["result"][:, feats],
                    scalar=0.0,
                    in1=h_sb[:, i, feats],
                    op0=ALU.max,
                    op1=ALU.add,
                )
                nc.sync.dma_start(out=out[i * P : (i + 1) * P, feats], in_=out_sb[:, feats])

        def is_tile(i):
            return 0 <= i < NODE_TILES


        flip_pair(k_mx, 0, psum_sc, "sc", nc.vector.tensor_copy)
        spread_bias()
        flip_pair(q_mx, 0, psum_sc, "sc")
        flip_pair(k_mx, 1, psum_sc, "sc")
        flip_pair(k_mx, 2, psum_sc, "sc")
        quantise_pair(k_mx, 0)
        flip_pair(k_mx, 3, psum_sc, "sc")
        quantise_pair(q_mx, 0)
        flip_pair(h_mx, 0, psum_tp, "tp")
        quantise_pair(k_mx, 1)
        flip_pair(h_mx, 1, psum_tp, "tp")
        score_half(0, 0)
        quantise_pair(k_mx, 2)
        quantise_pair(k_mx, 3)
        flip_pair(q_mx, 1, psum_tp, "tp")
        score_half(0, 1)
        half_maximum(0, 0)
        quantise_pair(h_mx, 0)
        half_maximum(0, 1)
        quantise_pair(h_mx, 1)
        flip_pair(wv_mx, 0, psum_tp, "tp")
        flip_pair(wv_mx, 1, psum_tp, "tp")

        flips = {1: [(q_mx, 2), (h_mx, 2)], 2: [(h_mx, 3)], 3: [(q_mx, 3)]}
        quants = {0: [(wv_mx, 0)], 2: [(h_mx, 2)]}
        banks = {1: [(0, 0), (0, 1)], 2: [(0, 2), (0, 3)], 3: [(1, 0), (1, 1)], 4: [(1, 2), (1, 3)]}
        quants1 = {0: [(q_mx, 1)], 1: [(wv_mx, 1)], 2: [(q_mx, 2)], 3: [(h_mx, 3)], 4: [(q_mx, 3)]}
        banks1 = {}
        vquants1 = {5: [1]}
        vquants = {3: [0]}

        for s in range(NODE_TILES + 0):
            for operand, pair in flips.get(s, []):
                flip_pair(operand, pair, psum_tp, "tp")
            if is_tile(s + 1):
                scores(s + 1)
            if 1 <= s < NODE_TILES:
                half_maximum(s - 0, 0)
            if 1 <= s < NODE_TILES:
                half_maximum(s - 0, 1)
            for job in quants1.get(s, []):
                quantise_pair(*job)
            for g in vquants1.get(s, []):
                quantise_values(g)
            if is_tile(s - 6):
                residual(s - 6)
            if is_tile(s - 1):
                sum_of_halves(s - 1)
            if is_tile(s - 0):
                shift_of(s - 0)
            if is_tile(s - 0):
                exponentials(s - 0)
            if is_tile(s - 5):
                quantise_attention(s - 5)
            if s == NODE_TILES - 1:
                quantise_attention(s - 4)
            for job in quants.get(s, []):
                quantise_pair(*job)
            for g in vquants.get(s, []):
                quantise_values(g)
            for g, c in banks1.get(s, []):
                value_bank(g, c)
            if is_tile(s - 1):
                inverse_of_sum(s - 1)
            if is_tile(s - 1):
                normalise(s - 1)
            for g, c in banks.get(s, []):
                value_bank(g, c)
            if is_tile(s - 2):
                lay_prior(s - 2)
                flip_attention(s - 2)
            if is_tile(s - 2):
                regroup(s - 2)
            if is_tile(s - 5):
                weighted_values(s - 5)

        weighted_values(3)
        lay_prior(6)
        flip_attention(6)
        regroup(6)
        quantise_attention(4)
        weighted_values(4)
        residual(2)
        sum_of_halves(7)
        residual(3)
        inverse_of_sum(7)
        quantise_attention(5)
        weighted_values(5)
        attention_half(7, 0)
        attention_half(7, 1)
        flip_finished_half(7, 0)
        regroup_half(7, 0)
        flip_finished_half(7, 1)
        regroup_half(7, 1)
        residual(4)
        quantise_attention(6)
        weighted_values(6)
        residual(5)
        quantise_half(7, 0)
        quantise_half(7, 1)
        weighted_half(7, 0)
        weighted_half(7, 1)
        residual(6)
        residual(7, 2)
